import numpy as np
import ml_dtypes


def mxq(x, axis, fmt="e4m3"):
    dtype, down = {"e4m3": (ml_dtypes.float8_e4m3fn, 7), "e5m2": (ml_dtypes.float8_e5m2, 14)}[fmt]
    v = np.moveaxis(np.asarray(x, np.float32).astype(ml_dtypes.bfloat16).astype(np.float64), axis, -1)
    blocks = v.reshape(v.shape[:-1] + (-1, 32))
    amax = np.abs(blocks).max(-1, keepdims=True)
    byte = np.maximum(np.where(amax > 0, np.frexp(amax)[1] - 1 + 127, 0) - down, 1)
    scale = np.exp2(byte - 127.0)
    codes = (blocks / scale).astype(np.float32).astype(dtype).astype(np.float64)
    return np.moveaxis((codes * scale).reshape(v.shape), -1, axis)


WIDE = False


def mx_kscale(k):
    if not WIDE:
        return np.ones(k)
    levels = np.array([10, -10, 5, -5, 0])
    a = np.random.permutation(np.resize(levels, k // 512 * 4)).reshape(k // 512, 4)
    idx = np.arange(k)
    return np.exp2(a[idx // 512, idx % 128 // 32])


BF16 = ml_dtypes.bfloat16


def bf(x):
    return np.asarray(x, np.float32).astype(BF16)


def f64(x):
    return np.asarray(x).astype(np.float64)


BATCH, WIDTH = 8192, 512


def _wide_factors():
    s = mx_kscale(WIDTH)[: WIDTH // 2]
    s = np.concatenate([s, s[::-1]])
    r = np.maximum(s, np.maximum(np.roll(s, 1), np.roll(s, -1)))
    return s, r


def setup_inputs():
    s, r = _wide_factors()
    x = np.random.standard_normal((BATCH, WIDTH)) * s
    W = np.random.standard_normal((WIDTH, WIDTH)) * (0.5 / np.sqrt(WIDTH)) * s.min() / (r[:, None] * r[None, :])
    return {'x': bf(x), 'W': bf(W)}


def _summed_permuted_weight(W):
    Ws = (
        np.rot90(W, k=1)
        + np.rot90(W, k=2)
        + np.rot90(W, k=3)
        + W.T
        + W[::-1, :]
        + W[:, ::-1]
        + W.T[::-1, ::-1]
        + np.roll(W, shift=1, axis=0)
        + np.roll(W, shift=1, axis=1)
    )
    return Ws


def reference(x, W):
    xq = mxq(f64(x), 1, 'e4m3')
    Wd = f64(W)
    reg_out = xq @ mxq(Wd.T, 0, 'e4m3')
    t_out = xq @ mxq(_summed_permuted_weight(Wd), 0, 'e4m3')
    return reg_out + t_out

@@ -1,0 +1,200 @@
+from contextlib import ExitStack
+
+import concourse.mybir as mybir
+from concourse.masks import make_identity
+
+F32 = mybir.dt.float32
+BF16 = mybir.dt.bfloat16
+U32 = mybir.dt.uint32
+U8 = mybir.dt.uint8
+FP8X4 = mybir.dt.float8_e4m3fn_x4
+NE = mybir.AluOpType.not_equal
+
+P = 128
+BATCH = 8192
+WIDTH = 512
+TILES = BATCH // P
+ROUND = 8
+ROUNDS = TILES // ROUND
+STORE = 4
+
+FLOPS = 2 * 2 * BATCH * WIDTH * WIDTH
+
+
+def tile_lin_transpose_t_kernel(tc, x, W, out):
+    nc = tc.nc
+    with ExitStack() as ctx:
+        const = ctx.enter_context(tc.tile_pool(name="const", bufs=1))
+        xin = ctx.enter_context(tc.tile_pool(name="xin", bufs=1))
+        xgp = ctx.enter_context(tc.tile_pool(name="xgp", bufs=2))
+        outp = ctx.enter_context(tc.tile_pool(name="outp", bufs=4))
+        psum = ctx.enter_context(tc.psum_pool(name="psum", bufs=1))
+        ctx.enter_context(tc.manual_schedule())
+
+        wpad = const.tile([P, 4, WIDTH + 2], BF16, name="wpad")
+        nc.sync.dma_start(out=wpad[:, :, 2 : WIDTH + 2], in_=W.rearrange("(p j) b -> p j b", j=4))
+        w2 = const.tile([P, 4 * WIDTH], BF16, name="w2")
+        nc.scalar.dma_start(
+            out=w2[:].rearrange("p (c b) -> p c b", c=4), in_=W.rearrange("(c p) b -> p c b", p=P)
+        )
+        x_flat = x.rearrange("(p t) k -> p (t k)", t=TILES)
+        out_flat = out.rearrange("(p t) n -> p (t n)", t=TILES)
+        x_sb = []
+        for r in range(ROUNDS):
+            xr = xin.tile([P, ROUND * WIDTH], BF16, name="x%d" % r)
+            nc.sync.dma_start(out=xr[:], in_=x_flat[:, r * ROUND * WIDTH : (r + 1) * ROUND * WIDTH])
+            x_sb.append(xr)
+
+        ident_f = const.tile([P, P], F32, name="ident_f")
+        make_identity(nc, ident_f[:])
+        flip_b = const.tile([P, P], BF16, name="flip_b")
+        nc.gpsimd.memset(flip_b[:], 0.0)
+        nc.gpsimd.affine_select(
+            out=flip_b[:], in_=flip_b[:], compare_op=NE, fill=1.0, base=-(P - 1),
+            pattern=[[1, P]], channel_multiplier=1,
+        )
+        ident_b = const.tile([P, P], BF16, name="ident_b")
+        make_identity(nc, ident_b[:])
+        shift_b = const.tile([P, P], BF16, name="shift_b")
+        nc.gpsimd.memset(shift_b[:], 0.0)
+        nc.gpsimd.affine_select(
+            out=shift_b[:], in_=shift_b[:], compare_op=NE, fill=1.0, base=1,
+            pattern=[[-1, P]], channel_multiplier=1,
+        )
+        nc.gpsimd.affine_select(
+            out=shift_b[:], in_=shift_b[:], compare_op=NE, fill=1.0, base=-(P - 1),
+            pattern=[[-1, P]], channel_multiplier=1,
+        )
+
+        w2w = w2[:].bitcast(F32).rearrange("p (c w u) -> p c u w", c=4, u=2)
+        h_ps = []
+        for h in range(2):
+            hp = psum.tile([P, 2, 256], F32, tag="b%d" % (4 + h), name="hps%d" % h)
+            for c2 in range(2):
+                for u in range(2):
+                    nc.tensor.transpose(hp[:, u, c2 * P : (c2 + 1) * P], w2w[:, 2 * h + c2, u, :], ident_f[:])
+            h_ps.append(hp)
+
+        nc.vector.tensor_copy(out=wpad[:, :, 1:2], in_=wpad[:, :, WIDTH + 1 : WIDTH + 2])
+        w_rev = const.tile([P, 4, WIDTH], BF16, name="w_rev")
+        nc.vector.tensor_copy(out=w_rev[:], in_=wpad[:, :, WIDTH + 1 : 1 : -1])
+
+        hw = const.tile([P, 2 * WIDTH], F32, name="hw")
+        hw_rev = const.tile([P, 2 * WIDTH], F32, name="hw_rev")
+        hg = const.tile([P, 4 * WIDTH], BF16, name="hg", align_bytes=64)
+        hw_v = hw[:].rearrange("p (u n) -> p u n", u=2)
+        hwr_v = hw_rev[:].rearrange("p (u n) -> p u n", u=2)
+        hg_v = hg[:].bitcast(F32).rearrange("p (n u) -> p n u", u=2)
+        for h in range(2):
+            cp = nc.vector.tensor_copy if h == 0 else nc.scalar.copy
+            cp(out=hg_v[:, 256 * h : 256 * (h + 1), :], in_=h_ps[h][:].rearrange("p u n -> p n u"))
+            cp(out=hw_v[:, :, 256 * h : 256 * (h + 1)], in_=h_ps[h][:])
+            cp(out=hwr_v[:, :, 256 * (1 - h) : 256 * (2 - h)], in_=h_ps[h][:, :, ::-1])
+        h_pl = hw[:].bitcast(BF16).rearrange("p (u n e) -> p u e n", u=2, e=2)
+        hr_pl = hw_rev[:].bitcast(BF16).rearrange("p (u n e) -> p u e n", u=2, e=2)
+
+        hq = const.tile([P, WIDTH], U32, name="hq", align_bytes=64)
+        hs = const.tile([P, WIDTH], U8, name="hs", align_bytes=64)
+        nc.vector.quantize_mx(out=hq[:].bitcast(FP8X4), scales=hs[:], in_=hg[:])
+
+        g_ps = [psum.tile([P, WIDTH], F32, tag="b%d" % t, name="gps%d" % t) for t in range(4)]
+        for t in range(4):
+            first = [
+                (flip_b, wpad[:, 3 - t, 2 : WIDTH + 2]),
+                (flip_b, w_rev[:, 3 - t, :]),
+                (ident_b, w_rev[:, t, :]),
+                (ident_b, wpad[:, t, 1 : WIDTH + 1]),
+                (ident_b, wpad[:, t - 1, 2 : WIDTH + 2]) if t > 0 else (shift_b, wpad[:, 3, 2 : WIDTH + 2]),
+            ]
+            for i, (lhs, rhs) in enumerate(first):
+                nc.tensor.matmul(g_ps[t][:], lhsT=lhs[:], rhs=rhs, start=(i == 0), stop=False)
+
+        x_w = [xr[:].bitcast(F32).rearrange("p (a w u) -> p a u w", a=ROUND, u=2) for xr in x_sb]
+
+        def transposes(r):
+            banks = []
+            for b in range(4):
+                xt = psum.tile([P, 2, 2, P], F32, tag="b%d" % (4 + b), name="xt%d_%d" % (r, b))
+                for a in range(2):
+                    for u in range(2):
+                        nc.tensor.transpose(xt[:, a, u, :], x_w[r][:, 2 * b + a, u, :], ident_f[:])
+                banks.append(xt)
+            return banks
+
+        def evacuate_x(banks, r):
+            xg = xgp.tile([P, ROUND * WIDTH], BF16, name="xg", align_bytes=64)
+            xg_v = xg[:].bitcast(F32).rearrange("p (b a r u) -> p b a r u", b=4, a=2, u=2)
+            for b in range(4):
+                nc.scalar.copy(out=xg_v[:, b], in_=banks[b][:].rearrange("p a u r -> p a r u"))
+            return xg
+
+        def quantise_x(xg, r):
+            xq = const.tile([P, ROUND * P], U32, name="xq%d" % r, align_bytes=64)
+            xs = const.tile([P, ROUND * P], U8, name="xs%d" % r, align_bytes=64)
+            for half in range(2):
+                nc.vector.quantize_mx(
+                    out=xq[:, 512 * half : 512 * (half + 1)].bitcast(FP8X4),
+                    scales=xs[:, 512 * half : 512 * (half + 1)],
+                    in_=xg[:, 2048 * half : 2048 * (half + 1)],
+                )
+            return xq, xs
+
+        banks = transposes(0)
+        xg = evacuate_x(banks, 0)
+        codes = {0: quantise_x(xg, 0)}
+
+        for t in range(4):
+            u, e = t // 2, t % 2
+            uf, ef = (3 - t) // 2, (3 - t) % 2
+            second = [
+                (ident_b, h_pl[:, u, e, :]),
+                (ident_b, hr_pl[:, u, e, :]),
+                (flip_b, h_pl[:, uf, ef, :]),
+                (flip_b, hr_pl[:, uf, ef, :]),
+            ]
+            for i, (lhs, rhs) in enumerate(second):
+                nc.tensor.matmul(g_ps[t][:], lhsT=lhs[:], rhs=rhs, start=False, stop=(i == 3))
+
+        g_pl = const.tile([P, 4, WIDTH], BF16, name="g_pl")
+        for t in range(4):
+            cp = nc.vector.tensor_copy if t < 2 else nc.scalar.copy
+            cp(out=g_pl[:, t, :], in_=g_ps[t][:])
+        gg = const.tile([P, WIDTH, 4], BF16, name="gg", align_bytes=64)
+        nc.vector.tensor_copy(
+            out=gg[:].rearrange("p (c i) t -> p c t i", i=4), in_=g_pl[:].rearrange("p t (c i) -> p c t i", i=4)
+        )
+        gq = const.tile([P, WIDTH], U32, name="gq", align_bytes=64)
+        gs = const.tile([P, WIDTH], U8, name="gs", align_bytes=64)
+        nc.vector.quantize_mx(out=gq[:].bitcast(FP8X4), scales=gs[:], in_=gg[:].rearrange("p n t -> p (n t)"))
+
+        for r in range(ROUNDS):
+            more = r + 1 < ROUNDS
+            if more:
+                banks = transposes(r + 1)
+                xg = evacuate_x(banks, r + 1)
+            xq, xs = codes[r]
+            o_sb = None
+            for i in range(ROUND):
+                acc = psum.tile([P, WIDTH], F32, tag="b%d" % (i % 4), name="acc%d_%d" % (r, i))
+                cols = slice(i * P, (i + 1) * P)
+                nc.tensor.matmul_mx(
+                    out=acc[:], lhsT=xq[:, cols].bitcast(FP8X4), lhsT_scale=xs[:, cols],
+                    rhs=hq[:].bitcast(FP8X4), rhs_scale=hs[:], start=True, stop=False,
+                )
+                nc.tensor.matmul_mx(
+                    out=acc[:], lhsT=xq[:, cols].bitcast(FP8X4), lhsT_scale=xs[:, cols],
+                    rhs=gq[:].bitcast(FP8X4), rhs_scale=gs[:], start=False, stop=True,
+                )
+                if i % STORE == 0:
+                    o_sb = outp.tile([P, STORE * WIDTH], F32, name="o_sb")
+                if more:
+                    on_vector = i < 4 or i == 7
+                else:
+                    on_vector = i % 2 == 0
+                cp = nc.vector.tensor_copy if on_vector else nc.scalar.copy
+                cp(out=o_sb[:, (i % STORE) * WIDTH : (i % STORE + 1) * WIDTH], in_=acc[:])
+                if more and i == 3:
+                    codes[r + 1] = quantise_x(xg, r + 1)
+                if i % STORE == STORE - 1:
+                    t0 = r * ROUND + i - (STORE - 1)
+                    nc.sync.dma_start(out=out_flat[:, t0 * WIDTH : (t0 + STORE) * WIDTH], in_=o_sb[:])

@@ -27,6 +27,7 @@ def tile_lin_transpose_t_kernel(tc, x, W, out):
         const = ctx.enter_context(tc.tile_pool(name="const", bufs=1))
         xin = ctx.enter_context(tc.tile_pool(name="xin", bufs=1))
         xgp = ctx.enter_context(tc.tile_pool(name="xgp", bufs=2))
+        xsp = ctx.enter_context(tc.tile_pool(name="xsp", bufs=3))
         outp = ctx.enter_context(tc.tile_pool(name="outp", bufs=4))
         psum = ctx.enter_context(tc.psum_pool(name="psum", bufs=1))
         ctx.enter_context(tc.manual_schedule())
@@ -111,13 +112,20 @@ def tile_lin_transpose_t_kernel(tc, x, W, out):
 
         x_w = [xr[:].bitcast(F32).rearrange("p (a w u) -> p a u w", a=ROUND, u=2) for xr in x_sb]
 
+        sorted_x = {}
+
+        def sort_words(r):
+            xo = xsp.tile([P, ROUND * 256], F32, name="xo")
+            nc.vector.tensor_copy(out=xo[:].rearrange("p (a u w) -> p a u w", a=ROUND, u=2), in_=x_w[r])
+            sorted_x[r] = xo[:].rearrange("p (a u w) -> p a u w", a=ROUND, u=2)
+
         def transposes(r):
             banks = []
             for b in range(4):
                 xt = psum.tile([P, 2, 2, P], F32, tag="b%d" % (4 + b), name="xt%d_%d" % (r, b))
                 for a in range(2):
                     for u in range(2):
-                        nc.tensor.transpose(xt[:, a, u, :], x_w[r][:, 2 * b + a, u, :], ident_f[:])
+                        nc.tensor.transpose(xt[:, a, u, :], sorted_x[r][:, 2 * b + a, u, :], ident_f[:])
                 banks.append(xt)
             return banks
 
@@ -139,6 +147,8 @@ def tile_lin_transpose_t_kernel(tc, x, W, out):
                 )
             return xq, xs
 
+        sort_words(0)
+        sort_words(1)
         banks = transposes(0)
         xg = evacuate_x(banks, 0)
         codes = {0: quantise_x(xg, 0)}
@@ -169,6 +179,8 @@ def tile_lin_transpose_t_kernel(tc, x, W, out):
 
         for r in range(ROUNDS):
             more = r + 1 < ROUNDS
+            if r + 2 < ROUNDS:
+                sort_words(r + 2)
             if more:
                 banks = transposes(r + 1)
                 xg = evacuate_x(banks, r + 1)
@@ -188,7 +200,7 @@ def tile_lin_transpose_t_kernel(tc, x, W, out):
                 if i % STORE == 0:
                     o_sb = outp.tile([P, STORE * WIDTH], F32, name="o_sb")
                 if more:
-                    on_vector = i < 4 or i == 7
+                    on_vector = i < 4
                 else:
                     on_vector = i % 2 == 0
                 cp = nc.vector.tensor_copy if on_vector else nc.scalar.copy

@@ -9,6 +9,7 @@ U32 = mybir.dt.uint32
 U8 = mybir.dt.uint8
 FP8X4 = mybir.dt.float8_e4m3fn_x4
 NE = mybir.AluOpType.not_equal
+ADD = mybir.AluOpType.add
 
 P = 128
 BATCH = 8192
@@ -77,41 +78,29 @@ def tile_lin_transpose_t_kernel(tc, x, W, out):
             h_ps.append(hp)
 
         nc.vector.tensor_copy(out=wpad[:, :, 1:2], in_=wpad[:, :, WIDTH + 1 : WIDTH + 2])
-        w_rev = const.tile([P, 4, WIDTH], BF16, name="w_rev")
-        nc.vector.tensor_copy(out=w_rev[:], in_=wpad[:, :, WIDTH + 1 : 1 : -1])
 
         hw = const.tile([P, 2 * WIDTH], F32, name="hw")
-        hw_rev = const.tile([P, 2 * WIDTH], F32, name="hw_rev")
         hg = const.tile([P, 4 * WIDTH], BF16, name="hg", align_bytes=64)
         hw_v = hw[:].rearrange("p (u n) -> p u n", u=2)
-        hwr_v = hw_rev[:].rearrange("p (u n) -> p u n", u=2)
         hg_v = hg[:].bitcast(F32).rearrange("p (n u) -> p n u", u=2)
         for h in range(2):
             cp = nc.vector.tensor_copy if h == 0 else nc.scalar.copy
-            cp(out=hg_v[:, 256 * h : 256 * (h + 1), :], in_=h_ps[h][:].rearrange("p u n -> p n u"))
             cp(out=hw_v[:, :, 256 * h : 256 * (h + 1)], in_=h_ps[h][:])
-            cp(out=hwr_v[:, :, 256 * (1 - h) : 256 * (2 - h)], in_=h_ps[h][:, :, ::-1])
+            cp(out=hg_v[:, 256 * h : 256 * (h + 1), :], in_=h_ps[h][:].rearrange("p u n -> p n u"))
         h_pl = hw[:].bitcast(BF16).rearrange("p (u n e) -> p u e n", u=2, e=2)
-        hr_pl = hw_rev[:].bitcast(BF16).rearrange("p (u n e) -> p u e n", u=2, e=2)
+
+        w_rev = const.tile([P, 4, WIDTH], BF16, name="w_rev")
+        nc.vector.tensor_copy(out=w_rev[:], in_=wpad[:, :, WIDTH + 1 : 1 : -1])
+
+        k_ps = [psum.tile([P, WIDTH], F32, tag="b%d" % t, name="kps%d" % t) for t in range(4)]
+        for t in range(4):
+            nc.tensor.matmul(k_ps[t][:], lhsT=flip_b[:], rhs=wpad[:, 3 - t, 2 : WIDTH + 2], start=True, stop=False)
 
         hq = const.tile([P, WIDTH], U32, name="hq", align_bytes=64)
         hs = const.tile([P, WIDTH], U8, name="hs", align_bytes=64)
         nc.vector.quantize_mx(out=hq[:].bitcast(FP8X4), scales=hs[:], in_=hg[:])
 
-        g_ps = [psum.tile([P, WIDTH], F32, tag="b%d" % t, name="gps%d" % t) for t in range(4)]
-        for t in range(4):
-            first = [
-                (flip_b, wpad[:, 3 - t, 2 : WIDTH + 2]),
-                (flip_b, w_rev[:, 3 - t, :]),
-                (ident_b, w_rev[:, t, :]),
-                (ident_b, wpad[:, t, 1 : WIDTH + 1]),
-                (ident_b, wpad[:, t - 1, 2 : WIDTH + 2]) if t > 0 else (shift_b, wpad[:, 3, 2 : WIDTH + 2]),
-            ]
-            for i, (lhs, rhs) in enumerate(first):
-                nc.tensor.matmul(g_ps[t][:], lhsT=lhs[:], rhs=rhs, start=(i == 0), stop=False)
-
         x_w = [xr[:].bitcast(F32).rearrange("p (a w u) -> p a u w", a=ROUND, u=2) for xr in x_sb]
-
         sorted_x = {}
 
         def sort_words(r):
@@ -122,7 +111,7 @@ def tile_lin_transpose_t_kernel(tc, x, W, out):
         def transposes(r):
             banks = []
             for b in range(4):
-                xt = psum.tile([P, 2, 2, P], F32, tag="b%d" % (4 + b), name="xt%d_%d" % (r, b))
+                xt = psum.tile([P, 2, 2, P], F32, tag="b%d" % b, name="xt%d_%d" % (r, b))
                 for a in range(2):
                     for u in range(2):
                         nc.tensor.transpose(xt[:, a, u, :], sorted_x[r][:, 2 * b + a, u, :], ident_f[:])
@@ -149,26 +138,32 @@ def tile_lin_transpose_t_kernel(tc, x, W, out):
 
         sort_words(0)
         sort_words(1)
-        banks = transposes(0)
-        xg = evacuate_x(banks, 0)
-        codes = {0: quantise_x(xg, 0)}
 
+        k_up = const.tile([P, 4, 256], F32, name="k_up")
+        k_sym = const.tile([P, 4, 256], F32, name="k_sym")
         for t in range(4):
-            u, e = t // 2, t % 2
-            uf, ef = (3 - t) // 2, (3 - t) % 2
-            second = [
-                (ident_b, h_pl[:, u, e, :]),
-                (ident_b, hr_pl[:, u, e, :]),
-                (flip_b, h_pl[:, uf, ef, :]),
-                (flip_b, hr_pl[:, uf, ef, :]),
-            ]
-            for i, (lhs, rhs) in enumerate(second):
-                nc.tensor.matmul(g_ps[t][:], lhsT=lhs[:], rhs=rhs, start=False, stop=(i == 3))
+            nc.tensor.matmul(k_ps[t][:], lhsT=ident_b[:], rhs=h_pl[:, t // 2, t % 2, :], start=False, stop=False)
+            nc.tensor.matmul(
+                k_ps[t][:], lhsT=flip_b[:], rhs=h_pl[:, (3 - t) // 2, (3 - t) % 2, :], start=False, stop=True
+            )
+            nc.scalar.copy(out=k_up[:, t, :], in_=k_ps[t][:, 256:512])
+            nc.vector.tensor_tensor(out=k_sym[:, t, :], in0=k_ps[t][:, 0:256], in1=k_up[:, t, ::-1], op=ADD)
 
         g_pl = const.tile([P, 4, WIDTH], BF16, name="g_pl")
         for t in range(4):
-            cp = nc.vector.tensor_copy if t < 2 else nc.scalar.copy
-            cp(out=g_pl[:, t, :], in_=g_ps[t][:])
+            l_ps = psum.tile([P, WIDTH], F32, tag="b%d" % (4 + t), name="lps%d" % t)
+            nc.tensor.matmul(l_ps[:], lhsT=ident_b[:], rhs=w_rev[:, t, :], start=True, stop=False)
+            nc.tensor.matmul(l_ps[:], lhsT=ident_b[:], rhs=wpad[:, t, 1 : WIDTH + 1], start=False, stop=False)
+            if t > 0:
+                nc.tensor.matmul(l_ps[:], lhsT=ident_b[:], rhs=wpad[:, t - 1, 2 : WIDTH + 2], start=False, stop=True)
+            else:
+                nc.tensor.matmul(l_ps[:], lhsT=shift_b[:], rhs=wpad[:, 3, 2 : WIDTH + 2], start=False, stop=True)
+            nc.vector.tensor_tensor(out=g_pl[:, t, 0:256], in0=l_ps[:, 0:256], in1=k_sym[:, t, :], op=ADD)
+            nc.vector.tensor_tensor(out=g_pl[:, t, 256:512], in0=l_ps[:, 256:512], in1=k_sym[:, t, ::-1], op=ADD)
+
+        banks = transposes(0)
+        xg = evacuate_x(banks, 0)
+
         gg = const.tile([P, WIDTH, 4], BF16, name="gg", align_bytes=64)
         nc.vector.tensor_copy(
             out=gg[:].rearrange("p (c i) t -> p c t i", i=4), in_=g_pl[:].rearrange("p t (c i) -> p c t i", i=4)
@@ -176,6 +171,7 @@ def tile_lin_transpose_t_kernel(tc, x, W, out):
         gq = const.tile([P, WIDTH], U32, name="gq", align_bytes=64)
         gs = const.tile([P, WIDTH], U8, name="gs", align_bytes=64)
         nc.vector.quantize_mx(out=gq[:].bitcast(FP8X4), scales=gs[:], in_=gg[:].rearrange("p n t -> p (n t)"))
+        codes = {0: quantise_x(xg, 0)}
 
         for r in range(ROUNDS):
             more = r + 1 < ROUNDS
@@ -187,7 +183,7 @@ def tile_lin_transpose_t_kernel(tc, x, W, out):
             xq, xs = codes[r]
             o_sb = None
             for i in range(ROUND):
-                acc = psum.tile([P, WIDTH], F32, tag="b%d" % (i % 4), name="acc%d_%d" % (r, i))
+                acc = psum.tile([P, WIDTH], F32, tag="b%d" % (4 + i % 4), name="acc%d_%d" % (r, i))
                 cols = slice(i * P, (i + 1) * P)
                 nc.tensor.matmul_mx(
                     out=acc[:], lhsT=xq[:, cols].bitcast(FP8X4), lhsT_scale=xs[:, cols],

@@ -14,10 +14,10 @@ ADD = mybir.AluOpType.add
 P = 128
 BATCH = 8192
 WIDTH = 512
+HALF = WIDTH // 2
 TILES = BATCH // P
 ROUND = 8
 ROUNDS = TILES // ROUND
-STORE = 4
 
 FLOPS = 2 * 2 * BATCH * WIDTH * WIDTH
 
@@ -33,12 +33,12 @@ def tile_lin_transpose_t_kernel(tc, x, W, out):
         psum = ctx.enter_context(tc.psum_pool(name="psum", bufs=1))
         ctx.enter_context(tc.manual_schedule())
 
-        wpad = const.tile([P, 4, WIDTH + 2], BF16, name="wpad")
-        nc.sync.dma_start(out=wpad[:, :, 2 : WIDTH + 2], in_=W.rearrange("(p j) b -> p j b", j=4))
         w2 = const.tile([P, 4 * WIDTH], BF16, name="w2")
-        nc.scalar.dma_start(
+        nc.sync.dma_start(
             out=w2[:].rearrange("p (c b) -> p c b", c=4), in_=W.rearrange("(c p) b -> p c b", p=P)
         )
+        wpad = const.tile([P, 4, WIDTH + 2], BF16, name="wpad")
+        nc.sync.dma_start(out=wpad[:, :, 2 : WIDTH + 2], in_=W.rearrange("(p j) b -> p j b", j=4))
         x_flat = x.rearrange("(p t) k -> p (t k)", t=TILES)
         out_flat = out.rearrange("(p t) n -> p (t n)", t=TILES)
         x_sb = []
@@ -71,13 +71,11 @@ def tile_lin_transpose_t_kernel(tc, x, W, out):
         w2w = w2[:].bitcast(F32).rearrange("p (c w u) -> p c u w", c=4, u=2)
         h_ps = []
         for h in range(2):
-            hp = psum.tile([P, 2, 256], F32, tag="b%d" % (4 + h), name="hps%d" % h)
+            hp = psum.tile([P, 2, HALF], F32, tag="b%d" % (4 + h), name="hps%d" % h)
             for c2 in range(2):
                 for u in range(2):
                     nc.tensor.transpose(hp[:, u, c2 * P : (c2 + 1) * P], w2w[:, 2 * h + c2, u, :], ident_f[:])
             h_ps.append(hp)
-
-        nc.vector.tensor_copy(out=wpad[:, :, 1:2], in_=wpad[:, :, WIDTH + 1 : WIDTH + 2])
 
         hw = const.tile([P, 2 * WIDTH], F32, name="hw")
         hg = const.tile([P, 4 * WIDTH], BF16, name="hg", align_bytes=64)
@@ -85,10 +83,11 @@ def tile_lin_transpose_t_kernel(tc, x, W, out):
         hg_v = hg[:].bitcast(F32).rearrange("p (n u) -> p n u", u=2)
         for h in range(2):
             cp = nc.vector.tensor_copy if h == 0 else nc.scalar.copy
-            cp(out=hw_v[:, :, 256 * h : 256 * (h + 1)], in_=h_ps[h][:])
-            cp(out=hg_v[:, 256 * h : 256 * (h + 1), :], in_=h_ps[h][:].rearrange("p u n -> p n u"))
+            cp(out=hw_v[:, :, HALF * h : HALF * (h + 1)], in_=h_ps[h][:])
+            cp(out=hg_v[:, HALF * h : HALF * (h + 1), :], in_=h_ps[h][:].rearrange("p u n -> p n u"))
         h_pl = hw[:].bitcast(BF16).rearrange("p (u n e) -> p u e n", u=2, e=2)
 
+        nc.vector.tensor_copy(out=wpad[:, :, 1:2], in_=wpad[:, :, WIDTH + 1 : WIDTH + 2])
         w_rev = const.tile([P, 4, WIDTH], BF16, name="w_rev")
         nc.vector.tensor_copy(out=w_rev[:], in_=wpad[:, :, WIDTH + 1 : 1 : -1])
 
@@ -100,13 +99,15 @@ def tile_lin_transpose_t_kernel(tc, x, W, out):
         hs = const.tile([P, WIDTH], U8, name="hs", align_bytes=64)
         nc.vector.quantize_mx(out=hq[:].bitcast(FP8X4), scales=hs[:], in_=hg[:])
 
-        x_w = [xr[:].bitcast(F32).rearrange("p (a w u) -> p a u w", a=ROUND, u=2) for xr in x_sb]
-        sorted_x = {}
+        x_src = {0: x_sb[0][:].bitcast(F32).rearrange("p (a w u) -> p a u w", a=ROUND, u=2)}
 
-        def sort_words(r):
-            xo = xsp.tile([P, ROUND * 256], F32, name="xo")
-            nc.vector.tensor_copy(out=xo[:].rearrange("p (a u w) -> p a u w", a=ROUND, u=2), in_=x_w[r])
-            sorted_x[r] = xo[:].rearrange("p (a u w) -> p a u w", a=ROUND, u=2)
+        def sort_words(r, cp):
+            xo = xsp.tile([P, ROUND * HALF], F32, name="xo")
+            cp(
+                out=xo[:].rearrange("p (a u w) -> p a u w", a=ROUND, u=2),
+                in_=x_sb[r][:].bitcast(F32).rearrange("p (a w u) -> p a u w", a=ROUND, u=2),
+            )
+            x_src[r] = xo[:].rearrange("p (a u w) -> p a u w", a=ROUND, u=2)
 
         def transposes(r):
             banks = []
@@ -114,11 +115,11 @@ def tile_lin_transpose_t_kernel(tc, x, W, out):
                 xt = psum.tile([P, 2, 2, P], F32, tag="b%d" % b, name="xt%d_%d" % (r, b))
                 for a in range(2):
                     for u in range(2):
-                        nc.tensor.transpose(xt[:, a, u, :], sorted_x[r][:, 2 * b + a, u, :], ident_f[:])
+                        nc.tensor.transpose(xt[:, a, u, :], x_src[r][:, 2 * b + a, u, :], ident_f[:])
                 banks.append(xt)
             return banks
 
-        def evacuate_x(banks, r):
+        def evacuate_x(banks):
             xg = xgp.tile([P, ROUND * WIDTH], BF16, name="xg", align_bytes=64)
             xg_v = xg[:].bitcast(F32).rearrange("p (b a r u) -> p b a r u", b=4, a=2, u=2)
             for b in range(4):
@@ -136,73 +137,105 @@ def tile_lin_transpose_t_kernel(tc, x, W, out):
                 )
             return xq, xs
 
-        sort_words(0)
-        sort_words(1)
-
-        k_up = const.tile([P, 4, 256], F32, name="k_up")
-        k_sym = const.tile([P, 4, 256], F32, name="k_sym")
+        k_up = const.tile([P, 4, HALF], F32, name="k_up")
+        k_sym = const.tile([P, 4, HALF], F32, name="k_sym")
         for t in range(4):
             nc.tensor.matmul(k_ps[t][:], lhsT=ident_b[:], rhs=h_pl[:, t // 2, t % 2, :], start=False, stop=False)
             nc.tensor.matmul(
                 k_ps[t][:], lhsT=flip_b[:], rhs=h_pl[:, (3 - t) // 2, (3 - t) % 2, :], start=False, stop=True
             )
-            nc.scalar.copy(out=k_up[:, t, :], in_=k_ps[t][:, 256:512])
-            nc.vector.tensor_tensor(out=k_sym[:, t, :], in0=k_ps[t][:, 0:256], in1=k_up[:, t, ::-1], op=ADD)
+            nc.scalar.copy(out=k_up[:, t, :], in_=k_ps[t][:, HALF:WIDTH])
+            nc.vector.tensor_tensor(out=k_sym[:, t, :], in0=k_ps[t][:, 0:HALF], in1=k_up[:, t, ::-1], op=ADD)
+        sort_words(1, nc.scalar.copy)
 
         g_pl = const.tile([P, 4, WIDTH], BF16, name="g_pl")
-        for t in range(4):
-            l_ps = psum.tile([P, WIDTH], F32, tag="b%d" % (4 + t), name="lps%d" % t)
-            nc.tensor.matmul(l_ps[:], lhsT=ident_b[:], rhs=w_rev[:, t, :], start=True, stop=False)
-            nc.tensor.matmul(l_ps[:], lhsT=ident_b[:], rhs=wpad[:, t, 1 : WIDTH + 1], start=False, stop=False)
-            if t > 0:
-                nc.tensor.matmul(l_ps[:], lhsT=ident_b[:], rhs=wpad[:, t - 1, 2 : WIDTH + 2], start=False, stop=True)
-            else:
-                nc.tensor.matmul(l_ps[:], lhsT=shift_b[:], rhs=wpad[:, 3, 2 : WIDTH + 2], start=False, stop=True)
-            nc.vector.tensor_tensor(out=g_pl[:, t, 0:256], in0=l_ps[:, 0:256], in1=k_sym[:, t, :], op=ADD)
-            nc.vector.tensor_tensor(out=g_pl[:, t, 256:512], in0=l_ps[:, 256:512], in1=k_sym[:, t, ::-1], op=ADD)
-
-        banks = transposes(0)
-        xg = evacuate_x(banks, 0)
-
         gg = const.tile([P, WIDTH, 4], BF16, name="gg", align_bytes=64)
-        nc.vector.tensor_copy(
-            out=gg[:].rearrange("p (c i) t -> p c t i", i=4), in_=g_pl[:].rearrange("p t (c i) -> p c t i", i=4)
-        )
         gq = const.tile([P, WIDTH], U32, name="gq", align_bytes=64)
         gs = const.tile([P, WIDTH], U8, name="gs", align_bytes=64)
-        nc.vector.quantize_mx(out=gq[:].bitcast(FP8X4), scales=gs[:], in_=gg[:].rearrange("p n t -> p (n t)"))
+
+        def finish_pair(half, pair):
+            lo = HALF * half
+            l_ps = psum.tile([P, 2, HALF], F32, tag="b%d" % (6 - 2 * half + pair), name="lps%d_%d" % (half, pair))
+            for e in range(2):
+                t = 2 * pair + e
+                nc.tensor.matmul(
+                    l_ps[:, e, :], lhsT=ident_b[:], rhs=wpad[:, t, 1 + lo : 1 + lo + HALF], start=True, stop=False
+                )
+                if t > 0:
+                    nc.tensor.matmul(
+                        l_ps[:, e, :], lhsT=ident_b[:], rhs=wpad[:, t - 1, 2 + lo : 2 + lo + HALF],
+                        start=False, stop=False,
+                    )
+                else:
+                    nc.tensor.matmul(
+                        l_ps[:, e, :], lhsT=shift_b[:], rhs=wpad[:, 3, 2 + lo : 2 + lo + HALF],
+                        start=False, stop=False,
+                    )
+                nc.tensor.matmul(
+                    l_ps[:, e, :], lhsT=ident_b[:], rhs=w_rev[:, t, lo : lo + HALF], start=False, stop=True
+                )
+            sym = k_sym[:, 2 * pair : 2 * pair + 2, :] if half == 0 else k_sym[:, 2 * pair : 2 * pair + 2, ::-1]
+            nc.vector.tensor_tensor(
+                out=g_pl[:, 2 * pair : 2 * pair + 2, lo : lo + HALF], in0=l_ps[:], in1=sym, op=ADD
+            )
+
+        def regroup(half):
+            lo = HALF * half
+            nc.vector.tensor_copy(
+                out=gg[:, lo : lo + HALF, :].rearrange("p (c i) t -> p c t i", i=4),
+                in_=g_pl[:, :, lo : lo + HALF].rearrange("p t (c i) -> p c t i", i=4),
+            )
+
+        def quantise_g(half):
+            lo = HALF * half
+            nc.vector.quantize_mx(
+                out=gq[:, lo : lo + HALF].bitcast(FP8X4), scales=gs[:, lo : lo + HALF],
+                in_=gg[:, lo : lo + HALF, :].rearrange("p n t -> p (n t)"),
+            )
+
+        finish_pair(0, 0)
+        finish_pair(0, 1)
+        regroup(0)
+        finish_pair(1, 0)
+        quantise_g(0)
+        finish_pair(1, 1)
+        regroup(1)
+        banks = transposes(0)
+        xg = evacuate_x(banks)
+        quantise_g(1)
         codes = {0: quantise_x(xg, 0)}
 
         for r in range(ROUNDS):
             more = r + 1 < ROUNDS
             if r + 2 < ROUNDS:
-                sort_words(r + 2)
+                sort_words(r + 2, nc.vector.tensor_copy)
             if more:
                 banks = transposes(r + 1)
-                xg = evacuate_x(banks, r + 1)
+                xg = evacuate_x(banks)
             xq, xs = codes[r]
-            o_sb = None
-            for i in range(ROUND):
-                acc = psum.tile([P, WIDTH], F32, tag="b%d" % (4 + i % 4), name="acc%d_%d" % (r, i))
-                cols = slice(i * P, (i + 1) * P)
-                nc.tensor.matmul_mx(
-                    out=acc[:], lhsT=xq[:, cols].bitcast(FP8X4), lhsT_scale=xs[:, cols],
-                    rhs=hq[:].bitcast(FP8X4), rhs_scale=hs[:], start=True, stop=False,
-                )
-                nc.tensor.matmul_mx(
-                    out=acc[:], lhsT=xq[:, cols].bitcast(FP8X4), lhsT_scale=xs[:, cols],
-                    rhs=gq[:].bitcast(FP8X4), rhs_scale=gs[:], start=False, stop=True,
-                )
-                if i % STORE == 0:
-                    o_sb = outp.tile([P, STORE * WIDTH], F32, name="o_sb")
-                if more:
-                    on_vector = i < 4
-                else:
-                    on_vector = i % 2 == 0
-                cp = nc.vector.tensor_copy if on_vector else nc.scalar.copy
-                cp(out=o_sb[:, (i % STORE) * WIDTH : (i % STORE + 1) * WIDTH], in_=acc[:])
-                if more and i == 3:
+            groups = [4, 4] if more else [4, 2, 1, 1]
+            i = 0
+            for size in groups:
+                o_sb = outp.tile([P, size * WIDTH], F32, name="o_sb")
+                for s in range(size):
+                    acc = psum.tile([P, WIDTH], F32, tag="b%d" % (4 + i % 4), name="acc%d_%d" % (r, i))
+                    cols = slice(i * P, (i + 1) * P)
+                    nc.tensor.matmul_mx(
+                        out=acc[:], lhsT=xq[:, cols].bitcast(FP8X4), lhsT_scale=xs[:, cols],
+                        rhs=hq[:].bitcast(FP8X4), rhs_scale=hs[:], start=True, stop=False,
+                    )
+                    nc.tensor.matmul_mx(
+                        out=acc[:], lhsT=xq[:, cols].bitcast(FP8X4), lhsT_scale=xs[:, cols],
+                        rhs=gq[:].bitcast(FP8X4), rhs_scale=gs[:], start=False, stop=True,
+                    )
+                    if more:
+                        on_vector = i < 4
+                    else:
+                        on_vector = i % 2 == 0
+                    cp = nc.vector.tensor_copy if on_vector else nc.scalar.copy
+                    cp(out=o_sb[:, s * WIDTH : (s + 1) * WIDTH], in_=acc[:])
+                    i += 1
+                if more and i == 4:
                     codes[r + 1] = quantise_x(xg, r + 1)
-                if i % STORE == STORE - 1:
-                    t0 = r * ROUND + i - (STORE - 1)
-                    nc.sync.dma_start(out=out_flat[:, t0 * WIDTH : (t0 + STORE) * WIDTH], in_=o_sb[:])
+                t0 = r * ROUND + i - size
+                nc.sync.dma_start(out=out_flat[:, t0 * WIDTH : (t0 + size) * WIDTH], in_=o_sb[:])

@@ -18,6 +18,7 @@ HALF = WIDTH // 2
 TILES = BATCH // P
 ROUND = 8
 ROUNDS = TILES // ROUND
+WARM = 6
 
 FLOPS = 2 * 2 * BATCH * WIDTH * WIDTH
 
@@ -46,6 +47,12 @@ def tile_lin_transpose_t_kernel(tc, x, W, out):
             xr = xin.tile([P, ROUND * WIDTH], BF16, name="x%d" % r)
             nc.sync.dma_start(out=xr[:], in_=x_flat[:, r * ROUND * WIDTH : (r + 1) * ROUND * WIDTH])
             x_sb.append(xr)
+
+        zeros = const.tile([P, WIDTH], BF16, name="zeros")
+        nc.vector.memset(zeros[:], 0.0)
+        warm = psum.tile([P, WIDTH], F32, tag="b7", name="warm")
+        for i in range(WARM):
+            nc.tensor.matmul(warm[:], lhsT=zeros[:, 0:P], rhs=zeros[:], start=True, stop=True)
 
         ident_f = const.tile([P, P], F32, name="ident_f")
         make_identity(nc, ident_f[:])

@@ -30,7 +30,7 @@ def tile_lin_transpose_t_kernel(tc, x, W, out):
         xin = ctx.enter_context(tc.tile_pool(name="xin", bufs=1))
         xgp = ctx.enter_context(tc.tile_pool(name="xgp", bufs=2))
         xsp = ctx.enter_context(tc.tile_pool(name="xsp", bufs=3))
-        outp = ctx.enter_context(tc.tile_pool(name="outp", bufs=4))
+        outp = ctx.enter_context(tc.tile_pool(name="outp", bufs=8))
         psum = ctx.enter_context(tc.psum_pool(name="psum", bufs=1))
         ctx.enter_context(tc.manual_schedule())
 
@@ -220,7 +220,7 @@ def tile_lin_transpose_t_kernel(tc, x, W, out):
                 banks = transposes(r + 1)
                 xg = evacuate_x(banks)
             xq, xs = codes[r]
-            groups = [4, 4] if more else [4, 2, 1, 1]
+            groups = [2, 2, 2, 2] if more else [2, 2, 2, 1, 1]
             i = 0
             for size in groups:
                 o_sb = outp.tile([P, size * WIDTH], F32, name="o_sb")

@@ -19,6 +19,7 @@ TILES = BATCH // P
 ROUND = 8
 ROUNDS = TILES // ROUND
 WARM = 6
+HEAD = 3
 
 FLOPS = 2 * 2 * BATCH * WIDTH * WIDTH
 
@@ -28,7 +29,7 @@ def tile_lin_transpose_t_kernel(tc, x, W, out):
     with ExitStack() as ctx:
         const = ctx.enter_context(tc.tile_pool(name="const", bufs=1))
         xin = ctx.enter_context(tc.tile_pool(name="xin", bufs=1))
-        xgp = ctx.enter_context(tc.tile_pool(name="xgp", bufs=2))
+        xgp = ctx.enter_context(tc.tile_pool(name="xgp", bufs=3))
         xsp = ctx.enter_context(tc.tile_pool(name="xsp", bufs=3))
         outp = ctx.enter_context(tc.tile_pool(name="outp", bufs=8))
         psum = ctx.enter_context(tc.psum_pool(name="psum", bufs=1))
@@ -38,8 +39,9 @@ def tile_lin_transpose_t_kernel(tc, x, W, out):
         nc.sync.dma_start(
             out=w2[:].rearrange("p (c b) -> p c b", c=4), in_=W.rearrange("(c p) b -> p c b", p=P)
         )
+        w_rows = W.rearrange("(p j) b -> p j b", j=4)
         wpad = const.tile([P, 4, WIDTH + 2], BF16, name="wpad")
-        nc.sync.dma_start(out=wpad[:, :, 2 : WIDTH + 2], in_=W.rearrange("(p j) b -> p j b", j=4))
+        nc.sync.dma_start(out=wpad[:, :, 2 : WIDTH + 2], in_=w_rows)
         x_flat = x.rearrange("(p t) k -> p (t k)", t=TILES)
         out_flat = out.rearrange("(p t) n -> p (t n)", t=TILES)
         x_sb = []
@@ -50,7 +52,7 @@ def tile_lin_transpose_t_kernel(tc, x, W, out):
 
         zeros = const.tile([P, WIDTH], BF16, name="zeros")
         nc.vector.memset(zeros[:], 0.0)
-        warm = psum.tile([P, WIDTH], F32, tag="b7", name="warm")
+        warm = psum.tile([P, WIDTH], F32, tag="b4", name="warm")
         for i in range(WARM):
             nc.tensor.matmul(warm[:], lhsT=zeros[:, 0:P], rhs=zeros[:], start=True, stop=True)
 
@@ -76,37 +78,53 @@ def tile_lin_transpose_t_kernel(tc, x, W, out):
         )
 
         w2w = w2[:].bitcast(F32).rearrange("p (c w u) -> p c u w", c=4, u=2)
-        h_ps = []
-        for h in range(2):
-            hp = psum.tile([P, 2, HALF], F32, tag="b%d" % (4 + h), name="hps%d" % h)
+        hg = const.tile([P, 4 * WIDTH], BF16, name="hg", align_bytes=64)
+        hg_w = hg[:].bitcast(F32).rearrange("p (c n u) -> p c n u", c=4, u=2)
+        for h, chunks in enumerate(((0, 3), (1, 2))):
+            hp = psum.tile([P, 2, 2, P], F32, tag="b%d" % (4 + h), name="hps%d" % h)
             for c2 in range(2):
                 for u in range(2):
-                    nc.tensor.transpose(hp[:, u, c2 * P : (c2 + 1) * P], w2w[:, 2 * h + c2, u, :], ident_f[:])
-            h_ps.append(hp)
-
-        hw = const.tile([P, 2 * WIDTH], F32, name="hw")
-        hg = const.tile([P, 4 * WIDTH], BF16, name="hg", align_bytes=64)
-        hw_v = hw[:].rearrange("p (u n) -> p u n", u=2)
-        hg_v = hg[:].bitcast(F32).rearrange("p (n u) -> p n u", u=2)
-        for h in range(2):
-            cp = nc.vector.tensor_copy if h == 0 else nc.scalar.copy
-            cp(out=hw_v[:, :, HALF * h : HALF * (h + 1)], in_=h_ps[h][:])
-            cp(out=hg_v[:, HALF * h : HALF * (h + 1), :], in_=h_ps[h][:].rearrange("p u n -> p n u"))
-        h_pl = hw[:].bitcast(BF16).rearrange("p (u n e) -> p u e n", u=2, e=2)
+                    nc.tensor.transpose(hp[:, u, c2, :], w2w[:, chunks[c2], u, :], ident_f[:])
+            cp = nc.scalar.copy
+            dst = hg_w[:, 0:4:3] if h == 0 else hg_w[:, 1:3]
+            cp(out=dst, in_=hp[:].rearrange("p u c n -> p c n u"))
+        t_pl = hg[:].rearrange("p (n t) -> p t n", t=4)
 
         nc.vector.tensor_copy(out=wpad[:, :, 1:2], in_=wpad[:, :, WIDTH + 1 : WIDTH + 2])
-        w_rev = const.tile([P, 4, WIDTH], BF16, name="w_rev")
-        nc.vector.tensor_copy(out=w_rev[:], in_=wpad[:, :, WIDTH + 1 : 1 : -1])
+        l1 = const.tile([P, 4, WIDTH], F32, name="l1")
+        l2 = const.tile([P, 4, WIDTH], F32, name="l2")
+        nc.vector.tensor_tensor(out=l1[:], in0=wpad[:, :, 1 : WIDTH + 1], in1=wpad[:, :, WIDTH + 1 : 1 : -1], op=ADD)
 
-        k_ps = [psum.tile([P, WIDTH], F32, tag="b%d" % t, name="kps%d" % t) for t in range(4)]
-        for t in range(4):
-            nc.tensor.matmul(k_ps[t][:], lhsT=flip_b[:], rhs=wpad[:, 3 - t, 2 : WIDTH + 2], start=True, stop=False)
+        w_val = wpad[:, :, 2 : WIDTH + 2]
+        ks = [psum.tile([P, 4, P], F32, tag="b%d" % (6 + b), name="ks%d" % b) for b in range(2)]
+
+        def fold_passes(b, perm, planes, first, last):
+            lo = P * b
+            hi = WIDTH - 1 - lo
+            nc.tensor.matmul(ks[b][:], lhsT=perm[:], rhs=planes[:, :, lo : lo + P], start=first, stop=False)
+            nc.tensor.matmul(ks[b][:], lhsT=perm[:], rhs=planes[:, :, hi : hi - P : -1], start=False, stop=last)
+
+        for b in range(2):
+            fold_passes(b, flip_b, w_val[:, ::-1, :], True, False)
+        up_ps = psum.tile([P, WIDTH], F32, tag="b3", name="up_ps")
+        nc.tensor.matmul(up_ps[:], lhsT=shift_b[:], rhs=w_val[:, 3, :], start=True, stop=True)
+        for b in range(2):
+            fold_passes(b, flip_b, t_pl[:, ::-1, :], False, False)
+            fold_passes(b, ident_b, t_pl, False, True)
+
+        nc.vector.tensor_tensor(out=l2[:, 0, :], in0=up_ps[:], in1=l1[:, 0, :], op=ADD)
+        nc.vector.tensor_tensor(out=l2[:, 1:4, :], in0=l1[:, 1:4, :], in1=w_val[:, 0:3, :], op=ADD)
 
         hq = const.tile([P, WIDTH], U32, name="hq", align_bytes=64)
         hs = const.tile([P, WIDTH], U8, name="hs", align_bytes=64)
-        nc.vector.quantize_mx(out=hq[:].bitcast(FP8X4), scales=hs[:], in_=hg[:])
+        gg = const.tile([P, WIDTH, 4], BF16, name="gg", align_bytes=64)
+        gq = const.tile([P, WIDTH], U32, name="gq", align_bytes=64)
+        gs = const.tile([P, WIDTH], U8, name="gs", align_bytes=64)
 
-        x_src = {0: x_sb[0][:].bitcast(F32).rearrange("p (a w u) -> p a u w", a=ROUND, u=2)}
+        x_src = {}
+
+        def unsorted(r):
+            x_src[r] = x_sb[r][:].bitcast(F32).rearrange("p (a w u) -> p a u w", a=ROUND, u=2)
 
         def sort_words(r, cp):
             xo = xsp.tile([P, ROUND * HALF], F32, name="xo")
@@ -133,6 +151,8 @@ def tile_lin_transpose_t_kernel(tc, x, W, out):
                 nc.scalar.copy(out=xg_v[:, b], in_=banks[b][:].rearrange("p a u r -> p a r u"))
             return xg
 
+        codes = {}
+
         def quantise_x(xg, r):
             xq = const.tile([P, ROUND * P], U32, name="xq%d" % r, align_bytes=64)
             xs = const.tile([P, ROUND * P], U8, name="xs%d" % r, align_bytes=64)
@@ -142,55 +162,18 @@ def tile_lin_transpose_t_kernel(tc, x, W, out):
                     scales=xs[:, 512 * half : 512 * (half + 1)],
                     in_=xg[:, 2048 * half : 2048 * (half + 1)],
                 )
-            return xq, xs
+            codes[r] = (xq, xs)
 
-        k_up = const.tile([P, 4, HALF], F32, name="k_up")
-        k_sym = const.tile([P, 4, HALF], F32, name="k_sym")
-        for t in range(4):
-            nc.tensor.matmul(k_ps[t][:], lhsT=ident_b[:], rhs=h_pl[:, t // 2, t % 2, :], start=False, stop=False)
-            nc.tensor.matmul(
-                k_ps[t][:], lhsT=flip_b[:], rhs=h_pl[:, (3 - t) // 2, (3 - t) % 2, :], start=False, stop=True
-            )
-            nc.scalar.copy(out=k_up[:, t, :], in_=k_ps[t][:, HALF:WIDTH])
-            nc.vector.tensor_tensor(out=k_sym[:, t, :], in0=k_ps[t][:, 0:HALF], in1=k_up[:, t, ::-1], op=ADD)
-        sort_words(1, nc.scalar.copy)
-
-        g_pl = const.tile([P, 4, WIDTH], BF16, name="g_pl")
-        gg = const.tile([P, WIDTH, 4], BF16, name="gg", align_bytes=64)
-        gq = const.tile([P, WIDTH], U32, name="gq", align_bytes=64)
-        gs = const.tile([P, WIDTH], U8, name="gs", align_bytes=64)
-
-        def finish_pair(half, pair):
-            lo = HALF * half
-            l_ps = psum.tile([P, 2, HALF], F32, tag="b%d" % (6 - 2 * half + pair), name="lps%d_%d" % (half, pair))
-            for e in range(2):
-                t = 2 * pair + e
-                nc.tensor.matmul(
-                    l_ps[:, e, :], lhsT=ident_b[:], rhs=wpad[:, t, 1 + lo : 1 + lo + HALF], start=True, stop=False
-                )
-                if t > 0:
-                    nc.tensor.matmul(
-                        l_ps[:, e, :], lhsT=ident_b[:], rhs=wpad[:, t - 1, 2 + lo : 2 + lo + HALF],
-                        start=False, stop=False,
-                    )
-                else:
-                    nc.tensor.matmul(
-                        l_ps[:, e, :], lhsT=shift_b[:], rhs=wpad[:, 3, 2 + lo : 2 + lo + HALF],
-                        start=False, stop=False,
-                    )
-                nc.tensor.matmul(
-                    l_ps[:, e, :], lhsT=ident_b[:], rhs=w_rev[:, t, lo : lo + HALF], start=False, stop=True
-                )
-            sym = k_sym[:, 2 * pair : 2 * pair + 2, :] if half == 0 else k_sym[:, 2 * pair : 2 * pair + 2, ::-1]
+        def finish(b, upper):
+            if upper:
+                cols = slice(WIDTH - P * (b + 1), WIDTH - P * b)
+                sym = ks[b][:, :, ::-1]
+            else:
+                cols = slice(P * b, P * (b + 1))
+                sym = ks[b][:]
             nc.vector.tensor_tensor(
-                out=g_pl[:, 2 * pair : 2 * pair + 2, lo : lo + HALF], in0=l_ps[:], in1=sym, op=ADD
-            )
-
-        def regroup(half):
-            lo = HALF * half
-            nc.vector.tensor_copy(
-                out=gg[:, lo : lo + HALF, :].rearrange("p (c i) t -> p c t i", i=4),
-                in_=g_pl[:, :, lo : lo + HALF].rearrange("p t (c i) -> p c t i", i=4),
+                out=gg[:, cols, :], in0=sym.rearrange("p t j -> p j t"),
+                in1=l2[:, :, cols].rearrange("p t j -> p j t"), op=ADD,
             )
 
         def quantise_g(half):
@@ -200,27 +183,34 @@ def tile_lin_transpose_t_kernel(tc, x, W, out):
                 in_=gg[:, lo : lo + HALF, :].rearrange("p n t -> p (n t)"),
             )
 
-        finish_pair(0, 0)
-        finish_pair(0, 1)
-        regroup(0)
-        finish_pair(1, 0)
+        xgs = {}
+        for r in range(HEAD):
+            unsorted(r)
+            xgs[r] = evacuate_x(transposes(r))
+        finish(0, False)
+        finish(1, False)
+        finish(1, True)
         quantise_g(0)
-        finish_pair(1, 1)
-        regroup(1)
-        banks = transposes(0)
-        xg = evacuate_x(banks)
+        finish(0, True)
+        nc.vector.quantize_mx(out=hq[:].bitcast(FP8X4), scales=hs[:], in_=hg[:])
         quantise_g(1)
-        codes = {0: quantise_x(xg, 0)}
+        quantise_x(xgs[0], 0)
 
         for r in range(ROUNDS):
-            more = r + 1 < ROUNDS
-            if r + 2 < ROUNDS:
+            last = r + 1 == ROUNDS
+            turn = r + 1 if HEAD <= r + 1 < ROUNDS else None
+            if HEAD <= r + 2 < ROUNDS:
                 sort_words(r + 2, nc.vector.tensor_copy)
-            if more:
-                banks = transposes(r + 1)
-                xg = evacuate_x(banks)
+            if turn:
+                xgs[turn] = evacuate_x(transposes(turn))
             xq, xs = codes[r]
-            groups = [2, 2, 2, 2] if more else [2, 2, 2, 1, 1]
+            groups = [2, 2, 2, 2] if not last else [2, 2, 2, 1, 1]
+            if turn:
+                on_vector = (0, 1, 2, 3)
+            elif last:
+                on_vector = (0, 2, 4, 6)
+            else:
+                on_vector = (0, 3, 6)
             i = 0
             for size in groups:
                 o_sb = outp.tile([P, size * WIDTH], F32, name="o_sb")
@@ -235,14 +225,10 @@ def tile_lin_transpose_t_kernel(tc, x, W, out):
                         out=acc[:], lhsT=xq[:, cols].bitcast(FP8X4), lhsT_scale=xs[:, cols],
                         rhs=gq[:].bitcast(FP8X4), rhs_scale=gs[:], start=False, stop=True,
                     )
-                    if more:
-                        on_vector = i < 4
-                    else:
-                        on_vector = i % 2 == 0
-                    cp = nc.vector.tensor_copy if on_vector else nc.scalar.copy
+                    cp = nc.vector.tensor_copy if i in on_vector else nc.scalar.copy
                     cp(out=o_sb[:, s * WIDTH : (s + 1) * WIDTH], in_=acc[:])
                     i += 1
-                if more and i == 4:
-                    codes[r + 1] = quantise_x(xg, r + 1)
+                if not last and i == 4:
+                    quantise_x(xgs[r + 1], r + 1)
                 t0 = r * ROUND + i - size
                 nc.sync.dma_start(out=out_flat[:, t0 * WIDTH : (t0 + size) * WIDTH], in_=o_sb[:])

@@ -19,6 +19,7 @@ TILES = BATCH // P
 ROUND = 8
 ROUNDS = TILES // ROUND
 WARM = 6
+KEEP = 2
 HEAD = 3
 
 FLOPS = 2 * 2 * BATCH * WIDTH * WIDTH
@@ -108,9 +109,14 @@ def tile_lin_transpose_t_kernel(tc, x, W, out):
             fold_passes(b, flip_b, w_val[:, ::-1, :], True, False)
         up_ps = psum.tile([P, WIDTH], F32, tag="b3", name="up_ps")
         nc.tensor.matmul(up_ps[:], lhsT=shift_b[:], rhs=w_val[:, 3, :], start=True, stop=True)
-        for b in range(2):
+
+        def fold_transposed(b):
             fold_passes(b, flip_b, t_pl[:, ::-1, :], False, False)
             fold_passes(b, ident_b, t_pl, False, True)
+
+        def keep_warm(n):
+            for i in range(n):
+                nc.tensor.matmul(warm2[:], lhsT=zeros[:, 0:P], rhs=zeros[:], start=True, stop=True)
 
         nc.vector.tensor_tensor(out=l2[:, 0, :], in0=up_ps[:], in1=l1[:, 0, :], op=ADD)
         nc.vector.tensor_tensor(out=l2[:, 1:4, :], in0=l1[:, 1:4, :], in1=w_val[:, 0:3, :], op=ADD)
@@ -186,15 +192,21 @@ def tile_lin_transpose_t_kernel(tc, x, W, out):
         xgs = {}
         for r in range(HEAD):
             unsorted(r)
-            xgs[r] = evacuate_x(transposes(r))
+        fold_transposed(0)
+        xgs[0] = evacuate_x(transposes(0))
+        fold_transposed(1)
+        xgs[1] = evacuate_x(transposes(1))
+        warm2 = psum.tile([P, WIDTH], F32, tag="b4", name="warm2")
+        keep_warm(KEEP)
+        xgs[2] = evacuate_x(transposes(2))
         finish(0, False)
-        finish(1, False)
-        finish(1, True)
-        quantise_g(0)
         finish(0, True)
+        finish(1, False)
         nc.vector.quantize_mx(out=hq[:].bitcast(FP8X4), scales=hs[:], in_=hg[:])
-        quantise_g(1)
+        quantise_g(0)
+        finish(1, True)
         quantise_x(xgs[0], 0)
+        quantise_g(1)
 
         for r in range(ROUNDS):
             last = r + 1 == ROUNDS

@@ -18,7 +18,8 @@ HALF = WIDTH // 2
 TILES = BATCH // P
 ROUND = 8
 ROUNDS = TILES // ROUND
-WARM = 6
+WARM = 4
+PLANE = WIDTH + 16
 KEEP = 2
 HEAD = 3
 
@@ -36,13 +37,10 @@ def tile_lin_transpose_t_kernel(tc, x, W, out):
         psum = ctx.enter_context(tc.psum_pool(name="psum", bufs=1))
         ctx.enter_context(tc.manual_schedule())
 
-        w2 = const.tile([P, 4 * WIDTH], BF16, name="w2")
-        nc.sync.dma_start(
-            out=w2[:].rearrange("p (c b) -> p c b", c=4), in_=W.rearrange("(c p) b -> p c b", p=P)
-        )
         w_rows = W.rearrange("(p j) b -> p j b", j=4)
-        wpad = const.tile([P, 4, WIDTH + 2], BF16, name="wpad")
-        nc.sync.dma_start(out=wpad[:, :, 2 : WIDTH + 2], in_=w_rows)
+        wpad = const.tile([P, 4, PLANE], BF16, name="wpad")
+        nc.sync.dma_start(out=wpad[:, 0:2, 2 : WIDTH + 2], in_=w_rows[:, 0:2, :])
+        nc.sync.dma_start(out=wpad[:, 2:4, 2 : WIDTH + 2], in_=w_rows[:, 2:4, :])
         x_flat = x.rearrange("(p t) k -> p (t k)", t=TILES)
         out_flat = out.rearrange("(p t) n -> p (t n)", t=TILES)
         x_sb = []
@@ -78,23 +76,28 @@ def tile_lin_transpose_t_kernel(tc, x, W, out):
             pattern=[[-1, P]], channel_multiplier=1,
         )
 
-        w2w = w2[:].bitcast(F32).rearrange("p (c w u) -> p c u w", c=4, u=2)
+        wp_w = wpad[:].bitcast(F32)
         hg = const.tile([P, 4 * WIDTH], BF16, name="hg", align_bytes=64)
-        hg_w = hg[:].bitcast(F32).rearrange("p (c n u) -> p c n u", c=4, u=2)
-        for h, chunks in enumerate(((0, 3), (1, 2))):
+        hg_w = hg[:].bitcast(F32).rearrange("p (n j u) -> p n j u", j=4, u=2)
+
+        def transpose_w(h):
             hp = psum.tile([P, 2, 2, P], F32, tag="b%d" % (4 + h), name="hps%d" % h)
-            for c2 in range(2):
+            for j in range(2):
                 for u in range(2):
-                    nc.tensor.transpose(hp[:, u, c2, :], w2w[:, chunks[c2], u, :], ident_f[:])
-            cp = nc.scalar.copy
-            dst = hg_w[:, 0:4:3] if h == 0 else hg_w[:, 1:3]
-            cp(out=dst, in_=hp[:].rearrange("p u c n -> p c n u"))
+                    nc.tensor.transpose(hp[:, j, u, :], wp_w[:, 2 * h + j, 1 + u : HALF + 1 : 2], ident_f[:])
+            nc.scalar.copy(out=hg_w[:, :, 2 * h : 2 * h + 2, :], in_=hp[:].rearrange("p j u n -> p n j u"))
+
+        transpose_w(0)
+        transpose_w(1)
         t_pl = hg[:].rearrange("p (n t) -> p t n", t=4)
 
-        nc.vector.tensor_copy(out=wpad[:, :, 1:2], in_=wpad[:, :, WIDTH + 1 : WIDTH + 2])
         l1 = const.tile([P, 4, WIDTH], F32, name="l1")
         l2 = const.tile([P, 4, WIDTH], F32, name="l2")
-        nc.vector.tensor_tensor(out=l1[:], in0=wpad[:, :, 1 : WIDTH + 1], in1=wpad[:, :, WIDTH + 1 : 1 : -1], op=ADD)
+        for s in (slice(0, 2), slice(2, 4)):
+            nc.vector.tensor_copy(out=wpad[:, s, 1:2], in_=wpad[:, s, WIDTH + 1 : WIDTH + 2])
+            nc.vector.tensor_tensor(
+                out=l1[:, s, :], in0=wpad[:, s, 1 : WIDTH + 1], in1=wpad[:, s, WIDTH + 1 : 1 : -1], op=ADD
+            )
 
         w_val = wpad[:, :, 2 : WIDTH + 2]
         ks = [psum.tile([P, 4, P], F32, tag="b%d" % (6 + b), name="ks%d" % b) for b in range(2)]
@@ -159,16 +162,21 @@ def tile_lin_transpose_t_kernel(tc, x, W, out):
 
         codes = {}
 
+        def quantise_half(xg, r, half):
+            if half == 0:
+                xq = const.tile([P, ROUND * P], U32, name="xq%d" % r, align_bytes=64)
+                xs = const.tile([P, ROUND * P], U8, name="xs%d" % r, align_bytes=64)
+                codes[r] = (xq, xs)
+            xq, xs = codes[r]
+            nc.vector.quantize_mx(
+                out=xq[:, 512 * half : 512 * (half + 1)].bitcast(FP8X4),
+                scales=xs[:, 512 * half : 512 * (half + 1)],
+                in_=xg[:, 2048 * half : 2048 * (half + 1)],
+            )
+
         def quantise_x(xg, r):
-            xq = const.tile([P, ROUND * P], U32, name="xq%d" % r, align_bytes=64)
-            xs = const.tile([P, ROUND * P], U8, name="xs%d" % r, align_bytes=64)
-            for half in range(2):
-                nc.vector.quantize_mx(
-                    out=xq[:, 512 * half : 512 * (half + 1)].bitcast(FP8X4),
-                    scales=xs[:, 512 * half : 512 * (half + 1)],
-                    in_=xg[:, 2048 * half : 2048 * (half + 1)],
-                )
-            codes[r] = (xq, xs)
+            quantise_half(xg, r, 0)
+            quantise_half(xg, r, 1)
 
         def finish(b, upper):
             if upper:
@@ -205,8 +213,9 @@ def tile_lin_transpose_t_kernel(tc, x, W, out):
         nc.vector.quantize_mx(out=hq[:].bitcast(FP8X4), scales=hs[:], in_=hg[:])
         quantise_g(0)
         finish(1, True)
-        quantise_x(xgs[0], 0)
+        quantise_half(xgs[0], 0, 0)
         quantise_g(1)
+        quantise_half(xgs[0], 0, 1)
 
         for r in range(ROUNDS):
             last = r + 1 == ROUNDS

@@ -34,6 +34,7 @@ def tile_lin_transpose_t_kernel(tc, x, W, out):
         xgp = ctx.enter_context(tc.tile_pool(name="xgp", bufs=3))
         xsp = ctx.enter_context(tc.tile_pool(name="xsp", bufs=3))
         outp = ctx.enter_context(tc.tile_pool(name="outp", bufs=8))
+        tailp = ctx.enter_context(tc.tile_pool(name="tailp", bufs=4))
         psum = ctx.enter_context(tc.psum_pool(name="psum", bufs=1))
         ctx.enter_context(tc.manual_schedule())
 
@@ -225,7 +226,7 @@ def tile_lin_transpose_t_kernel(tc, x, W, out):
             if turn:
                 xgs[turn] = evacuate_x(transposes(turn))
             xq, xs = codes[r]
-            groups = [2, 2, 2, 2] if not last else [2, 2, 2, 1, 1]
+            groups = [2, 2, 2, 2] if not last else [2, 2, 2, 1]
             if turn:
                 on_vector = (0, 1, 2, 3)
             elif last:
@@ -253,3 +254,22 @@ def tile_lin_transpose_t_kernel(tc, x, W, out):
                     quantise_x(xgs[r + 1], r + 1)
                 t0 = r * ROUND + i - size
                 nc.sync.dma_start(out=out_flat[:, t0 * WIDTH : (t0 + size) * WIDTH], in_=o_sb[:])
+
+        xq, xs = codes[ROUNDS - 1]
+        cols = slice((ROUND - 1) * P, ROUND * P)
+        for q in range(4):
+            piece = slice(q * P, (q + 1) * P)
+            acc = psum.tile([P, P], F32, tag="b%d" % q, name="tail%d" % q)
+            nc.tensor.matmul_mx(
+                out=acc[:], lhsT=xq[:, cols].bitcast(FP8X4), lhsT_scale=xs[:, cols],
+                rhs=hq[:, piece].bitcast(FP8X4), rhs_scale=hs[:, piece], start=True, stop=False,
+            )
+            nc.tensor.matmul_mx(
+                out=acc[:], lhsT=xq[:, cols].bitcast(FP8X4), lhsT_scale=xs[:, cols],
+                rhs=gq[:, piece].bitcast(FP8X4), rhs_scale=gs[:, piece], start=False, stop=True,
+            )
+            o_q = tailp.tile([P, P], F32, name="o_q")
+            cp = nc.vector.tensor_copy if q % 2 == 0 else nc.scalar.copy
+            cp(out=o_q[:], in_=acc[:])
+            lo = (TILES - 1) * WIDTH + q * P
+            nc.sync.dma_start(out=out_flat[:, lo : lo + P], in_=o_q[:])

@@ -20,7 +20,6 @@ ROUND = 8
 ROUNDS = TILES // ROUND
 WARM = 4
 PLANE = WIDTH + 16
-KEEP = 2
 HEAD = 3
 
 FLOPS = 2 * 2 * BATCH * WIDTH * WIDTH
@@ -47,7 +46,13 @@ def tile_lin_transpose_t_kernel(tc, x, W, out):
         x_sb = []
         for r in range(ROUNDS):
             xr = xin.tile([P, ROUND * WIDTH], BF16, name="x%d" % r)
-            nc.sync.dma_start(out=xr[:], in_=x_flat[:, r * ROUND * WIDTH : (r + 1) * ROUND * WIDTH])
+            parts = 2 if r == 0 else 1
+            step = ROUND * WIDTH // parts
+            for h in range(parts):
+                nc.sync.dma_start(
+                    out=xr[:, h * step : (h + 1) * step],
+                    in_=x_flat[:, r * ROUND * WIDTH + h * step : r * ROUND * WIDTH + (h + 1) * step],
+                )
             x_sb.append(xr)
 
         zeros = const.tile([P, WIDTH], BF16, name="zeros")
@@ -118,10 +123,6 @@ def tile_lin_transpose_t_kernel(tc, x, W, out):
             fold_passes(b, flip_b, t_pl[:, ::-1, :], False, False)
             fold_passes(b, ident_b, t_pl, False, True)
 
-        def keep_warm(n):
-            for i in range(n):
-                nc.tensor.matmul(warm2[:], lhsT=zeros[:, 0:P], rhs=zeros[:], start=True, stop=True)
-
         nc.vector.tensor_tensor(out=l2[:, 0, :], in0=up_ps[:], in1=l1[:, 0, :], op=ADD)
         nc.vector.tensor_tensor(out=l2[:, 1:4, :], in0=l1[:, 1:4, :], in1=w_val[:, 0:3, :], op=ADD)
 
@@ -142,6 +143,18 @@ def tile_lin_transpose_t_kernel(tc, x, W, out):
                 out=xo[:].rearrange("p (a u w) -> p a u w", a=ROUND, u=2),
                 in_=x_sb[r][:].bitcast(F32).rearrange("p (a w u) -> p a u w", a=ROUND, u=2),
             )
+            x_src[r] = xo[:].rearrange("p (a u w) -> p a u w", a=ROUND, u=2)
+
+        def sort_halves(r, cp):
+            xo = xsp.tile([P, ROUND * HALF], F32, name="xo")
+            half = ROUND // 2
+            for h in range(2):
+                cp(
+                    out=xo[:, h * half * HALF : (h + 1) * half * HALF].rearrange("p (a u w) -> p a u w", a=half, u=2),
+                    in_=x_sb[r][:, h * half * WIDTH : (h + 1) * half * WIDTH].bitcast(F32).rearrange(
+                        "p (a w u) -> p a u w", a=half, u=2
+                    ),
+                )
             x_src[r] = xo[:].rearrange("p (a u w) -> p a u w", a=ROUND, u=2)
 
         def transposes(r):
@@ -199,24 +212,40 @@ def tile_lin_transpose_t_kernel(tc, x, W, out):
             )
 
         xgs = {}
-        for r in range(HEAD):
-            unsorted(r)
+        sort_halves(0, nc.scalar.copy)
+        unsorted(1)
+        unsorted(2)
         fold_transposed(0)
         xgs[0] = evacuate_x(transposes(0))
-        fold_transposed(1)
+        fold_passes(1, flip_b, t_pl[:, ::-1, :], False, False)
         xgs[1] = evacuate_x(transposes(1))
-        warm2 = psum.tile([P, WIDTH], F32, tag="b4", name="warm2")
-        keep_warm(KEEP)
+        fold_passes(1, ident_b, t_pl, False, True)
         xgs[2] = evacuate_x(transposes(2))
         finish(0, False)
         finish(0, True)
-        finish(1, False)
         nc.vector.quantize_mx(out=hq[:].bitcast(FP8X4), scales=hs[:], in_=hg[:])
-        quantise_g(0)
-        finish(1, True)
         quantise_half(xgs[0], 0, 0)
+        finish(1, False)
+        finish(1, True)
+        quantise_g(0)
         quantise_g(1)
         quantise_half(xgs[0], 0, 1)
+
+        accs = {}
+
+        def mx_pass(r, i, second):
+            xq, xs = codes[r]
+            cols = slice(i * P, (i + 1) * P)
+            if not second:
+                accs[i] = psum.tile([P, WIDTH], F32, tag="b%d" % (4 + i % 4), name="acc%d_%d" % (r, i))
+            wq, ws = (gq, gs) if second else (hq, hs)
+            nc.tensor.matmul_mx(
+                out=accs[i][:], lhsT=xq[:, cols].bitcast(FP8X4), lhsT_scale=xs[:, cols],
+                rhs=wq[:].bitcast(FP8X4), rhs_scale=ws[:], start=not second, stop=second,
+            )
+
+        for i in range(4):
+            mx_pass(0, i, False)
 
         for r in range(ROUNDS):
             last = r + 1 == ROUNDS
@@ -225,7 +254,6 @@ def tile_lin_transpose_t_kernel(tc, x, W, out):
                 sort_words(r + 2, nc.vector.tensor_copy)
             if turn:
                 xgs[turn] = evacuate_x(transposes(turn))
-            xq, xs = codes[r]
             groups = [2, 2, 2, 2] if not last else [2, 2, 2, 1]
             if turn:
                 on_vector = (0, 1, 2, 3)
@@ -237,18 +265,11 @@ def tile_lin_transpose_t_kernel(tc, x, W, out):
             for size in groups:
                 o_sb = outp.tile([P, size * WIDTH], F32, name="o_sb")
                 for s in range(size):
-                    acc = psum.tile([P, WIDTH], F32, tag="b%d" % (4 + i % 4), name="acc%d_%d" % (r, i))
-                    cols = slice(i * P, (i + 1) * P)
-                    nc.tensor.matmul_mx(
-                        out=acc[:], lhsT=xq[:, cols].bitcast(FP8X4), lhsT_scale=xs[:, cols],
-                        rhs=hq[:].bitcast(FP8X4), rhs_scale=hs[:], start=True, stop=False,
-                    )
-                    nc.tensor.matmul_mx(
-                        out=acc[:], lhsT=xq[:, cols].bitcast(FP8X4), lhsT_scale=xs[:, cols],
-                        rhs=gq[:].bitcast(FP8X4), rhs_scale=gs[:], start=False, stop=True,
-                    )
+                    if r > 0 or i >= 4:
+                        mx_pass(r, i, False)
+                    mx_pass(r, i, True)
                     cp = nc.vector.tensor_copy if i in on_vector else nc.scalar.copy
-                    cp(out=o_sb[:, s * WIDTH : (s + 1) * WIDTH], in_=acc[:])
+                    cp(out=o_sb[:, s * WIDTH : (s + 1) * WIDTH], in_=accs[i][:])
                     i += 1
                 if not last and i == 4:
                     quantise_x(xgs[r + 1], r + 1)

@@ -255,14 +255,9 @@ def tile_lin_transpose_t_kernel(tc, x, W, out):
             if turn:
                 xgs[turn] = evacuate_x(transposes(turn))
             groups = [2, 2, 2, 2] if not last else [2, 2, 2, 1]
-            if turn:
-                on_vector = (0, 1, 2, 3)
-            elif last:
-                on_vector = (0, 2, 4, 6)
-            else:
-                on_vector = (0, 3, 6)
+            on_vector = (0, 1, 4, 5) if turn or last else (0, 1)
             i = 0
-            for size in groups:
+            for g, size in enumerate(groups):
                 o_sb = outp.tile([P, size * WIDTH], F32, name="o_sb")
                 for s in range(size):
                     if r > 0 or i >= 4:
@@ -274,7 +269,8 @@ def tile_lin_transpose_t_kernel(tc, x, W, out):
                 if not last and i == 4:
                     quantise_x(xgs[r + 1], r + 1)
                 t0 = r * ROUND + i - size
-                nc.sync.dma_start(out=out_flat[:, t0 * WIDTH : (t0 + size) * WIDTH], in_=o_sb[:])
+                queue = nc.sync if g % 2 == 0 else nc.scalar
+                queue.dma_start(out=out_flat[:, t0 * WIDTH : (t0 + size) * WIDTH], in_=o_sb[:])
 
         xq, xs = codes[ROUNDS - 1]
         cols = slice((ROUND - 1) * P, ROUND * P)
@@ -293,4 +289,5 @@ def tile_lin_transpose_t_kernel(tc, x, W, out):
             cp = nc.vector.tensor_copy if q % 2 == 0 else nc.scalar.copy
             cp(out=o_q[:], in_=acc[:])
             lo = (TILES - 1) * WIDTH + q * P
-            nc.sync.dma_start(out=out_flat[:, lo : lo + P], in_=o_q[:])
+            queue = nc.sync if q % 2 == 0 else nc.scalar
+            queue.dma_start(out=out_flat[:, lo : lo + P], in_=o_q[:])

@@ -237,7 +237,11 @@ def tile_lin_transpose_t_kernel(tc, x, W, out):
             xq, xs = codes[r]
             cols = slice(i * P, (i + 1) * P)
             if not second:
-                accs[i] = psum.tile([P, WIDTH], F32, tag="b%d" % (4 + i % 4), name="acc%d_%d" % (r, i))
+                if i in (4, 5):
+                    bank = i - 2
+                else:
+                    bank = 4 + (6 * r + (i if i < 4 else i - 2)) % 4
+                accs[i] = psum.tile([P, WIDTH], F32, tag="b%d" % bank, name="acc%d_%d" % (r, i))
             wq, ws = (gq, gs) if second else (hq, hs)
             nc.tensor.matmul_mx(
                 out=accs[i][:], lhsT=xq[:, cols].bitcast(FP8X4), lhsT_scale=xs[:, cols],

@@ -116,15 +116,15 @@ def tile_lin_transpose_t_kernel(tc, x, W, out):
 
         for b in range(2):
             fold_passes(b, flip_b, w_val[:, ::-1, :], True, False)
-        up_ps = psum.tile([P, WIDTH], F32, tag="b3", name="up_ps")
+        up_ps = psum.tile([P, WIDTH], F32, tag="b5", name="up_ps")
         nc.tensor.matmul(up_ps[:], lhsT=shift_b[:], rhs=w_val[:, 3, :], start=True, stop=True)
 
         def fold_transposed(b):
             fold_passes(b, flip_b, t_pl[:, ::-1, :], False, False)
             fold_passes(b, ident_b, t_pl, False, True)
 
-        nc.vector.tensor_tensor(out=l2[:, 0, :], in0=up_ps[:], in1=l1[:, 0, :], op=ADD)
         nc.vector.tensor_tensor(out=l2[:, 1:4, :], in0=l1[:, 1:4, :], in1=w_val[:, 0:3, :], op=ADD)
+        nc.vector.tensor_tensor(out=l2[:, 0, :], in0=up_ps[:], in1=l1[:, 0, :], op=ADD)
 
         hq = const.tile([P, WIDTH], U32, name="hq", align_bytes=64)
         hs = const.tile([P, WIDTH], U8, name="hs", align_bytes=64)
@@ -214,16 +214,16 @@ def tile_lin_transpose_t_kernel(tc, x, W, out):
         xgs = {}
         sort_halves(0, nc.scalar.copy)
         unsorted(1)
-        unsorted(2)
         fold_transposed(0)
         xgs[0] = evacuate_x(transposes(0))
         fold_passes(1, flip_b, t_pl[:, ::-1, :], False, False)
         xgs[1] = evacuate_x(transposes(1))
         fold_passes(1, ident_b, t_pl, False, True)
-        xgs[2] = evacuate_x(transposes(2))
         finish(0, False)
         finish(0, True)
         nc.vector.quantize_mx(out=hq[:].bitcast(FP8X4), scales=hs[:], in_=hg[:])
+        sort_halves(2, nc.vector.tensor_copy)
+        xgs[2] = evacuate_x(transposes(2))
         quantise_half(xgs[0], 0, 0)
         finish(1, False)
         finish(1, True)
@@ -258,7 +258,7 @@ def tile_lin_transpose_t_kernel(tc, x, W, out):
                 sort_words(r + 2, nc.vector.tensor_copy)
             if turn:
                 xgs[turn] = evacuate_x(transposes(turn))
-            groups = [2, 2, 2, 2] if not last else [2, 2, 2, 1]
+            groups = [2, 2, 2, 2] if r + 2 < ROUNDS else [1] * 8 if not last else [1] * 7
             on_vector = (0, 1, 4, 5) if turn or last else (0, 1)
             i = 0
             for g, size in enumerate(groups):
@@ -273,7 +273,7 @@ def tile_lin_transpose_t_kernel(tc, x, W, out):
                 if not last and i == 4:
                     quantise_x(xgs[r + 1], r + 1)
                 t0 = r * ROUND + i - size
-                queue = nc.sync if g % 2 == 0 else nc.scalar
+                queue = nc.sync if i - 1 in on_vector else nc.scalar
                 queue.dma_start(out=out_flat[:, t0 * WIDTH : (t0 + size) * WIDTH], in_=o_sb[:])
 
         xq, xs = codes[ROUNDS - 1]

@@ -258,8 +258,8 @@ def tile_lin_transpose_t_kernel(tc, x, W, out):
                 sort_words(r + 2, nc.vector.tensor_copy)
             if turn:
                 xgs[turn] = evacuate_x(transposes(turn))
-            groups = [2, 2, 2, 2] if r + 2 < ROUNDS else [1] * 8 if not last else [1] * 7
-            on_vector = (0, 1, 4, 5) if turn or last else (0, 1)
+            groups = [2, 2, 2, 2] if not last else [2, 2, 2, 1]
+            on_vector = (0, 1, 4, 5)
             i = 0
             for g, size in enumerate(groups):
                 o_sb = outp.tile([P, size * WIDTH], F32, name="o_sb")
@@ -270,10 +270,10 @@ def tile_lin_transpose_t_kernel(tc, x, W, out):
                     cp = nc.vector.tensor_copy if i in on_vector else nc.scalar.copy
                     cp(out=o_sb[:, s * WIDTH : (s + 1) * WIDTH], in_=accs[i][:])
                     i += 1
-                if not last and i == 4:
-                    quantise_x(xgs[r + 1], r + 1)
+                if not last and i in (4, 6):
+                    quantise_half(xgs[r + 1], r + 1, i // 2 - 2)
                 t0 = r * ROUND + i - size
-                queue = nc.sync if i - 1 in on_vector else nc.scalar
+                queue = nc.sync if g % 2 == 0 else nc.scalar
                 queue.dma_start(out=out_flat[:, t0 * WIDTH : (t0 + size) * WIDTH], in_=o_sb[:])
 
         xq, xs = codes[ROUNDS - 1]

@@ -32,8 +32,7 @@ def tile_lin_transpose_t_kernel(tc, x, W, out):
         xin = ctx.enter_context(tc.tile_pool(name="xin", bufs=1))
         xgp = ctx.enter_context(tc.tile_pool(name="xgp", bufs=3))
         xsp = ctx.enter_context(tc.tile_pool(name="xsp", bufs=3))
-        outp = ctx.enter_context(tc.tile_pool(name="outp", bufs=8))
-        tailp = ctx.enter_context(tc.tile_pool(name="tailp", bufs=4))
+        outp = ctx.enter_context(tc.tile_pool(name="outp", bufs=5))
         psum = ctx.enter_context(tc.psum_pool(name="psum", bufs=1))
         ctx.enter_context(tc.manual_schedule())
 
@@ -258,7 +257,7 @@ def tile_lin_transpose_t_kernel(tc, x, W, out):
                 sort_words(r + 2, nc.vector.tensor_copy)
             if turn:
                 xgs[turn] = evacuate_x(transposes(turn))
-            groups = [2, 2, 2, 2] if not last else [2, 2, 2, 1]
+            groups = [4, 4] if r < ROUNDS // 2 else [2, 2, 2, 2]
             on_vector = (0, 1, 4, 5)
             i = 0
             for g, size in enumerate(groups):
@@ -270,28 +269,8 @@ def tile_lin_transpose_t_kernel(tc, x, W, out):
                     cp = nc.vector.tensor_copy if i in on_vector else nc.scalar.copy
                     cp(out=o_sb[:, s * WIDTH : (s + 1) * WIDTH], in_=accs[i][:])
                     i += 1
-                if not last and i in (4, 6):
-                    quantise_half(xgs[r + 1], r + 1, i // 2 - 2)
+                    if not last and i in (4, 6):
+                        quantise_half(xgs[r + 1], r + 1, i // 2 - 2)
                 t0 = r * ROUND + i - size
                 queue = nc.sync if g % 2 == 0 else nc.scalar
                 queue.dma_start(out=out_flat[:, t0 * WIDTH : (t0 + size) * WIDTH], in_=o_sb[:])
-
-        xq, xs = codes[ROUNDS - 1]
-        cols = slice((ROUND - 1) * P, ROUND * P)
-        for q in range(4):
-            piece = slice(q * P, (q + 1) * P)
-            acc = psum.tile([P, P], F32, tag="b%d" % q, name="tail%d" % q)
-            nc.tensor.matmul_mx(
-                out=acc[:], lhsT=xq[:, cols].bitcast(FP8X4), lhsT_scale=xs[:, cols],
-                rhs=hq[:, piece].bitcast(FP8X4), rhs_scale=hs[:, piece], start=True, stop=False,
-            )
-            nc.tensor.matmul_mx(
-                out=acc[:], lhsT=xq[:, cols].bitcast(FP8X4), lhsT_scale=xs[:, cols],
-                rhs=gq[:, piece].bitcast(FP8X4), rhs_scale=gs[:, piece], start=False, stop=True,
-            )
-            o_q = tailp.tile([P, P], F32, name="o_q")
-            cp = nc.vector.tensor_copy if q % 2 == 0 else nc.scalar.copy
-            cp(out=o_q[:], in_=acc[:])
-            lo = (TILES - 1) * WIDTH + q * P
-            queue = nc.sync if q % 2 == 0 else nc.scalar
-            queue.dma_start(out=out_flat[:, lo : lo + P], in_=o_q[:])

from contextlib import ExitStack

import concourse.mybir as mybir
from concourse.masks import make_identity

F32 = mybir.dt.float32
BF16 = mybir.dt.bfloat16
U32 = mybir.dt.uint32
U8 = mybir.dt.uint8
FP8X4 = mybir.dt.float8_e4m3fn_x4
NE = mybir.AluOpType.not_equal
ADD = mybir.AluOpType.add

P = 128
BATCH = 8192
WIDTH = 512
HALF = WIDTH // 2
TILES = BATCH // P
ROUND = 8
ROUNDS = TILES // ROUND
WARM = 4
PLANE = WIDTH + 16
HEAD = 3

FLOPS = 2 * 2 * BATCH * WIDTH * WIDTH


def tile_lin_transpose_t_kernel(tc, x, W, out):
    nc = tc.nc
    with ExitStack() as ctx:
        const = ctx.enter_context(tc.tile_pool(name="const", bufs=1))
        xin = ctx.enter_context(tc.tile_pool(name="xin", bufs=1))
        xgp = ctx.enter_context(tc.tile_pool(name="xgp", bufs=3))
        xsp = ctx.enter_context(tc.tile_pool(name="xsp", bufs=3))
        outp = ctx.enter_context(tc.tile_pool(name="outp", bufs=5))
        psum = ctx.enter_context(tc.psum_pool(name="psum", bufs=1))
        ctx.enter_context(tc.manual_schedule())

        w_rows = W.rearrange("(p j) b -> p j b", j=4)
        wpad = const.tile([P, 4, PLANE], BF16, name="wpad")
        nc.sync.dma_start(out=wpad[:, 0:2, 2 : WIDTH + 2], in_=w_rows[:, 0:2, :])
        nc.sync.dma_start(out=wpad[:, 2:4, 2 : WIDTH + 2], in_=w_rows[:, 2:4, :])
        x_flat = x.rearrange("(p t) k -> p (t k)", t=TILES)
        out_flat = out.rearrange("(p t) n -> p (t n)", t=TILES)
        x_sb = []
        for r in range(ROUNDS):
            xr = xin.tile([P, ROUND * WIDTH], BF16, name="x%d" % r)
            parts = 2 if r == 0 else 1
            step = ROUND * WIDTH // parts
            for h in range(parts):
                nc.sync.dma_start(
                    out=xr[:, h * step : (h + 1) * step],
                    in_=x_flat[:, r * ROUND * WIDTH + h * step : r * ROUND * WIDTH + (h + 1) * step],
                )
            x_sb.append(xr)

        zeros = const.tile([P, WIDTH], BF16, name="zeros")
        nc.vector.memset(zeros[:], 0.0)
        warm = psum.tile([P, WIDTH], F32, tag="b4", name="warm")
        for i in range(WARM):
            nc.tensor.matmul(warm[:], lhsT=zeros[:, 0:P], rhs=zeros[:], start=True, stop=True)

        ident_f = const.tile([P, P], F32, name="ident_f")
        make_identity(nc, ident_f[:])
        flip_b = const.tile([P, P], BF16, name="flip_b")
        nc.gpsimd.memset(flip_b[:], 0.0)
        nc.gpsimd.affine_select(
            out=flip_b[:], in_=flip_b[:], compare_op=NE, fill=1.0, base=-(P - 1),
            pattern=[[1, P]], channel_multiplier=1,
        )
        ident_b = const.tile([P, P], BF16, name="ident_b")
        make_identity(nc, ident_b[:])
        shift_b = const.tile([P, P], BF16, name="shift_b")
        nc.gpsimd.memset(shift_b[:], 0.0)
        nc.gpsimd.affine_select(
            out=shift_b[:], in_=shift_b[:], compare_op=NE, fill=1.0, base=1,
            pattern=[[-1, P]], channel_multiplier=1,
        )
        nc.gpsimd.affine_select(
            out=shift_b[:], in_=shift_b[:], compare_op=NE, fill=1.0, base=-(P - 1),
            pattern=[[-1, P]], channel_multiplier=1,
        )

        wp_w = wpad[:].bitcast(F32)
        hg = const.tile([P, 4 * WIDTH], BF16, name="hg", align_bytes=64)
        hg_w = hg[:].bitcast(F32).rearrange("p (n j u) -> p n j u", j=4, u=2)

        def transpose_w(h):
            hp = psum.tile([P, 2, 2, P], F32, tag="b%d" % (4 + h), name="hps%d" % h)
            for j in range(2):
                for u in range(2):
                    nc.tensor.transpose(hp[:, j, u, :], wp_w[:, 2 * h + j, 1 + u : HALF + 1 : 2], ident_f[:])
            nc.scalar.copy(out=hg_w[:, :, 2 * h : 2 * h + 2, :], in_=hp[:].rearrange("p j u n -> p n j u"))

        transpose_w(0)
        transpose_w(1)
        t_pl = hg[:].rearrange("p (n t) -> p t n", t=4)

        l1 = const.tile([P, 4, WIDTH], F32, name="l1")
        l2 = const.tile([P, 4, WIDTH], F32, name="l2")
        for s in (slice(0, 2), slice(2, 4)):
            nc.vector.tensor_copy(out=wpad[:, s, 1:2], in_=wpad[:, s, WIDTH + 1 : WIDTH + 2])
            nc.vector.tensor_tensor(
                out=l1[:, s, :], in0=wpad[:, s, 1 : WIDTH + 1], in1=wpad[:, s, WIDTH + 1 : 1 : -1], op=ADD
            )

        w_val = wpad[:, :, 2 : WIDTH + 2]
        ks = [psum.tile([P, 4, P], F32, tag="b%d" % (6 + b), name="ks%d" % b) for b in range(2)]

        def fold_passes(b, perm, planes, first, last):
            lo = P * b
            hi = WIDTH - 1 - lo
            nc.tensor.matmul(ks[b][:], lhsT=perm[:], rhs=planes[:, :, lo : lo + P], start=first, stop=False)
            nc.tensor.matmul(ks[b][:], lhsT=perm[:], rhs=planes[:, :, hi : hi - P : -1], start=False, stop=last)

        for b in range(2):
            fold_passes(b, flip_b, w_val[:, ::-1, :], True, False)
        up_ps = psum.tile([P, WIDTH], F32, tag="b5", name="up_ps")
        nc.tensor.matmul(up_ps[:], lhsT=shift_b[:], rhs=w_val[:, 3, :], start=True, stop=True)

        def fold_transposed(b):
            fold_passes(b, flip_b, t_pl[:, ::-1, :], False, False)
            fold_passes(b, ident_b, t_pl, False, True)

        nc.vector.tensor_tensor(out=l2[:, 1:4, :], in0=l1[:, 1:4, :], in1=w_val[:, 0:3, :], op=ADD)
        nc.vector.tensor_tensor(out=l2[:, 0, :], in0=up_ps[:], in1=l1[:, 0, :], op=ADD)

        hq = const.tile([P, WIDTH], U32, name="hq", align_bytes=64)
        hs = const.tile([P, WIDTH], U8, name="hs", align_bytes=64)
        gg = const.tile([P, WIDTH, 4], BF16, name="gg", align_bytes=64)
        gq = const.tile([P, WIDTH], U32, name="gq", align_bytes=64)
        gs = const.tile([P, WIDTH], U8, name="gs", align_bytes=64)

        x_src = {}

        def unsorted(r):
            x_src[r] = x_sb[r][:].bitcast(F32).rearrange("p (a w u) -> p a u w", a=ROUND, u=2)

        def sort_words(r, cp):
            xo = xsp.tile([P, ROUND * HALF], F32, name="xo")
            cp(
                out=xo[:].rearrange("p (a u w) -> p a u w", a=ROUND, u=2),
                in_=x_sb[r][:].bitcast(F32).rearrange("p (a w u) -> p a u w", a=ROUND, u=2),
            )
            x_src[r] = xo[:].rearrange("p (a u w) -> p a u w", a=ROUND, u=2)

        def sort_halves(r, cp):
            xo = xsp.tile([P, ROUND * HALF], F32, name="xo")
            half = ROUND // 2
            for h in range(2):
                cp(
                    out=xo[:, h * half * HALF : (h + 1) * half * HALF].rearrange("p (a u w) -> p a u w", a=half, u=2),
                    in_=x_sb[r][:, h * half * WIDTH : (h + 1) * half * WIDTH].bitcast(F32).rearrange(
                        "p (a w u) -> p a u w", a=half, u=2
                    ),
                )
            x_src[r] = xo[:].rearrange("p (a u w) -> p a u w", a=ROUND, u=2)

        def transposes(r):
            banks = []
            for b in range(4):
                xt = psum.tile([P, 2, 2, P], F32, tag="b%d" % b, name="xt%d_%d" % (r, b))
                for a in range(2):
                    for u in range(2):
                        nc.tensor.transpose(xt[:, a, u, :], x_src[r][:, 2 * b + a, u, :], ident_f[:])
                banks.append(xt)
            return banks

        def evacuate_x(banks):
            xg = xgp.tile([P, ROUND * WIDTH], BF16, name="xg", align_bytes=64)
            xg_v = xg[:].bitcast(F32).rearrange("p (b a r u) -> p b a r u", b=4, a=2, u=2)
            for b in range(4):
                nc.scalar.copy(out=xg_v[:, b], in_=banks[b][:].rearrange("p a u r -> p a r u"))
            return xg

        codes = {}

        def quantise_half(xg, r, half):
            if half == 0:
                xq = const.tile([P, ROUND * P], U32, name="xq%d" % r, align_bytes=64)
                xs = const.tile([P, ROUND * P], U8, name="xs%d" % r, align_bytes=64)
                codes[r] = (xq, xs)
            xq, xs = codes[r]
            nc.vector.quantize_mx(
                out=xq[:, 512 * half : 512 * (half + 1)].bitcast(FP8X4),
                scales=xs[:, 512 * half : 512 * (half + 1)],
                in_=xg[:, 2048 * half : 2048 * (half + 1)],
            )

        def quantise_x(xg, r):
            quantise_half(xg, r, 0)
            quantise_half(xg, r, 1)

        def finish(b, upper):
            if upper:
                cols = slice(WIDTH - P * (b + 1), WIDTH - P * b)
                sym = ks[b][:, :, ::-1]
            else:
                cols = slice(P * b, P * (b + 1))
                sym = ks[b][:]
            nc.vector.tensor_tensor(
                out=gg[:, cols, :], in0=sym.rearrange("p t j -> p j t"),
                in1=l2[:, :, cols].rearrange("p t j -> p j t"), op=ADD,
            )

        def quantise_g(half):
            lo = HALF * half
            nc.vector.quantize_mx(
                out=gq[:, lo : lo + HALF].bitcast(FP8X4), scales=gs[:, lo : lo + HALF],
                in_=gg[:, lo : lo + HALF, :].rearrange("p n t -> p (n t)"),
            )

        xgs = {}
        sort_halves(0, nc.scalar.copy)
        unsorted(1)
        fold_transposed(0)
        xgs[0] = evacuate_x(transposes(0))
        fold_passes(1, flip_b, t_pl[:, ::-1, :], False, False)
        xgs[1] = evacuate_x(transposes(1))
        fold_passes(1, ident_b, t_pl, False, True)
        finish(0, False)
        finish(0, True)
        nc.vector.quantize_mx(out=hq[:].bitcast(FP8X4), scales=hs[:], in_=hg[:])
        sort_halves(2, nc.vector.tensor_copy)
        xgs[2] = evacuate_x(transposes(2))
        quantise_half(xgs[0], 0, 0)
        finish(1, False)
        finish(1, True)
        quantise_g(0)
        quantise_g(1)
        quantise_half(xgs[0], 0, 1)

        accs = {}

        def mx_pass(r, i, second):
            xq, xs = codes[r]
            cols = slice(i * P, (i + 1) * P)
            if not second:
                if i in (4, 5):
                    bank = i - 2
                else:
                    bank = 4 + (6 * r + (i if i < 4 else i - 2)) % 4
                accs[i] = psum.tile([P, WIDTH], F32, tag="b%d" % bank, name="acc%d_%d" % (r, i))
            wq, ws = (gq, gs) if second else (hq, hs)
            nc.tensor.matmul_mx(
                out=accs[i][:], lhsT=xq[:, cols].bitcast(FP8X4), lhsT_scale=xs[:, cols],
                rhs=wq[:].bitcast(FP8X4), rhs_scale=ws[:], start=not second, stop=second,
            )

        for i in range(4):
            mx_pass(0, i, False)

        for r in range(ROUNDS):
            last = r + 1 == ROUNDS
            turn = r + 1 if HEAD <= r + 1 < ROUNDS else None
            if HEAD <= r + 2 < ROUNDS:
                sort_words(r + 2, nc.vector.tensor_copy)
            if turn:
                xgs[turn] = evacuate_x(transposes(turn))
            groups = [4, 4] if r < ROUNDS // 2 else [2, 2, 2, 2]
            on_vector = (0, 1, 4, 5)
            i = 0
            for g, size in enumerate(groups):
                o_sb = outp.tile([P, size * WIDTH], F32, name="o_sb")
                for s in range(size):
                    if r > 0 or i >= 4:
                        mx_pass(r, i, False)
                    mx_pass(r, i, True)
                    cp = nc.vector.tensor_copy if i in on_vector else nc.scalar.copy
                    cp(out=o_sb[:, s * WIDTH : (s + 1) * WIDTH], in_=accs[i][:])
                    i += 1
                    if not last and i in (4, 6):
                        quantise_half(xgs[r + 1], r + 1, i // 2 - 2)
                t0 = r * ROUND + i - size
                queue = nc.sync if g % 2 == 0 else nc.scalar
                queue.dma_start(out=out_flat[:, t0 * WIDTH : (t0 + size) * WIDTH], in_=o_sb[:])
